import numpy as np
import ml_dtypes


def mxq(x, axis, fmt="e4m3"):
    dtype, down = {"e4m3": (ml_dtypes.float8_e4m3fn, 7), "e5m2": (ml_dtypes.float8_e5m2, 14)}[fmt]
    v = np.moveaxis(np.asarray(x, np.float32).astype(ml_dtypes.bfloat16).astype(np.float64), axis, -1)
    blocks = v.reshape(v.shape[:-1] + (-1, 32))
    amax = np.abs(blocks).max(-1, keepdims=True)
    byte = np.maximum(np.where(amax > 0, np.frexp(amax)[1] - 1 + 127, 0) - down, 1)
    scale = np.exp2(byte - 127.0)
    codes = (blocks / scale).astype(np.float32).astype(dtype).astype(np.float64)
    return np.moveaxis((codes * scale).reshape(v.shape), -1, axis)


WIDE = False


def mx_kscale(k):
    if not WIDE:
        return np.ones(k)
    levels = np.array([10, -10, 5, -5, 0])
    a = np.random.permutation(np.resize(levels, k // 512 * 4)).reshape(k // 512, 4)
    idx = np.arange(k)
    return np.exp2(a[idx // 512, idx % 128 // 32])


BF16 = ml_dtypes.bfloat16


def bf(x):
    return np.asarray(x, np.float32).astype(BF16)


def f64(x):
    return np.asarray(x).astype(np.float64)


B, CIN, HID, FREQ, T, H = 4, 1024, 128, 4, 512, 8
HD = HID * FREQ // H
EPS = 1e-5


def setup_inputs():
    s = mx_kscale(CIN)
    return {"x": bf(np.random.standard_normal((B, CIN, FREQ, T)) * s[None, :, None, None]),
            "qkv_w": bf(np.random.standard_normal((3 * HID, CIN)) / np.sqrt(CIN) / s[None, :]),
            "qkv_b": bf(np.random.standard_normal(3 * HID) * 0.2),
            "qkv_alpha": bf(0.25 + 0.05 * np.random.standard_normal(1)),
            "qkv_gamma": bf(1.0 + 0.1 * np.random.standard_normal((1, 3 * HID, 1, FREQ))),
            "qkv_beta": bf(0.1 * np.random.standard_normal((1, 3 * HID, 1, FREQ)))}


def reference(x, qkv_w, qkv_b, qkv_alpha, qkv_gamma, qkv_beta):
    xt = np.swapaxes(f64(x), -2, -1)
    y = (mxq(f64(qkv_w), 1, "e4m3") @ mxq(xt, 1, "e4m3").reshape(B, CIN, T * FREQ)).reshape(B, 3 * HID, T, FREQ)
    y = y + f64(qkv_b)[None, :, None, None]
    y = np.where(y >= 0, y, f64(qkv_alpha)[0] * y)
    mu = y.mean(axis=(1, 3), keepdims=True)
    var = np.square(y - mu).mean(axis=(1, 3), keepdims=True)
    n = (y - mu) / np.sqrt(var + EPS) * f64(qkv_gamma) + f64(qkv_beta)
    n = np.swapaxes(np.swapaxes(n, 1, 2).reshape(B, T, H, 3 * HD), 1, 2)
    return (np.ascontiguousarray(n[..., :HD]), np.ascontiguousarray(n[..., HD:2 * HD]), np.ascontiguousarray(n[..., 2 * HD:]))

@@ -1,0 +1,375 @@
+from contextlib import ExitStack
+
+import concourse.mybir as mybir
+from concourse.masks import make_identity
+
+F32 = mybir.dt.float32
+BF16 = mybir.dt.bfloat16
+U32 = mybir.dt.uint32
+U8 = mybir.dt.uint8
+FP8X4 = mybir.dt.float8_e4m3fn_x4
+ALU = mybir.AluOpType
+ACT = mybir.ActivationFunctionType
+
+B, CIN, HID, FREQ, T, H = 4, 1024, 128, 4, 512, 8
+OUT_CH = 3 * HID
+HD = HID * FREQ // H
+EPS = 1e-5
+
+P = 128
+PACK = 4
+K_PASS = P * PACK
+PASSES = CIN // K_PASS
+PAIRS = PACK // 2
+O_STRIPES = OUT_CH // P
+T_STRIPES = T // P
+UNITS = B * T_STRIPES
+COLS = OUT_CH * FREQ
+BANK = 512
+BANKS = COLS // BANK
+HEAD_COLS = COLS // H
+
+LAST_PIECES = 4
+
+EARLY_STEPS = 96
+RUN = 4
+
+FLOPS = 2 * OUT_CH * CIN * B * FREQ * T
+
+ROW_BIAS = 0
+ROW_ALPHA = OUT_CH
+ROW_GAMMA = BANK
+ROW_BETA = BANK + COLS
+ROW_COLS = BANK + 2 * COLS
+
+
+def tile_unified2dattentiononframe_pa_t_kernel(
+    tc, x, qkv_w, qkv_b, qkv_alpha, qkv_gamma, qkv_beta, out_0, out_1, out_2
+):
+    nc = tc.nc
+    outs = (out_0, out_1, out_2)
+    with ExitStack() as ctx:
+        const = ctx.enter_context(tc.tile_pool(name="const", bufs=1))
+        raw_pool = ctx.enter_context(tc.tile_pool(name="raw", bufs=2 * PASSES))
+        grouped_pool = ctx.enter_context(tc.tile_pool(name="grouped", bufs=2))
+        grouped_late_pool = ctx.enter_context(tc.tile_pool(name="grouped_late", bufs=1))
+        code_pool = ctx.enter_context(tc.tile_pool(name="codes", bufs=3))
+        slope_pool = ctx.enter_context(tc.tile_pool(name="slope", bufs=2))
+        p_pool = ctx.enter_context(tc.tile_pool(name="p", bufs=2))
+        n_pool = ctx.enter_context(tc.tile_pool(name="n", bufs=4))
+        small = ctx.enter_context(tc.tile_pool(name="small", bufs=4))
+        square_pool = ctx.enter_context(tc.tile_pool(name="square", bufs=2))
+        z_pool = ctx.enter_context(tc.psum_pool(name="z", bufs=BANKS))
+        pt_pool = ctx.enter_context(tc.psum_pool(name="pt", bufs=BANKS))
+        setup_pool = ctx.enter_context(tc.psum_pool(name="setup", bufs=2))
+        ctx.enter_context(tc.manual_schedule())
+
+        raw = {}
+
+        def new_x_tiles(b):
+            for g in range(PASSES):
+                chunk = raw_pool.tile([P, PACK, FREQ, T], BF16, tag="raw", name="chunk")
+                raw[(b, g)] = chunk
+
+        def load_x(b, t_range):
+            for g in range(PASSES):
+                nc.sync.dma_start(
+                    out=raw[(b, g)][:, :, :, t_range],
+                    in_=x[b, g * K_PASS : (g + 1) * K_PASS, :, t_range].rearrange("(p j) f t -> p j f t", j=PACK),
+                )
+
+        rows = const.tile([P, ROW_COLS], BF16)
+        nc.vector.memset(rows[:], 0.0)
+        ones = const.tile([P, P], BF16)
+        nc.vector.memset(ones[:], 1.0)
+        eps_t = const.tile([P, 1], F32)
+        nc.vector.memset(eps_t[:], EPS)
+        w_sb = const.tile([P, O_STRIPES * CIN], BF16)
+        nc.sync.dma_start(
+            out=w_sb[:].rearrange("p (a c) -> p a c", a=O_STRIPES),
+            in_=qkv_w.rearrange("(a p) c -> p a c", p=P),
+        )
+        new_x_tiles(0)
+        load_x(0, slice(0, P))
+        nc.sync.dma_start(out=rows[0:1, ROW_ALPHA : ROW_ALPHA + 1], in_=qkv_alpha.rearrange("(r o) -> r o", r=1))
+        nc.sync.dma_start(out=rows[0:1, ROW_BIAS : ROW_BIAS + OUT_CH], in_=qkv_b.rearrange("(r o) -> r o", r=1))
+        nc.sync.dma_start(out=rows[0:1, ROW_GAMMA : ROW_GAMMA + COLS], in_=qkv_gamma.rearrange("r o c f -> r (o c f)"))
+        nc.sync.dma_start(out=rows[0:1, ROW_BETA : ROW_BETA + COLS], in_=qkv_beta.rearrange("r o c f -> r (o c f)"))
+        for tt in range(1, T_STRIPES):
+            load_x(0, slice(tt * P, (tt + 1) * P))
+        new_x_tiles(1)
+        load_x(1, slice(0, T))
+
+        warm = const.tile([P, 1], F32)
+        nc.scalar.activation(out=warm[:], in_=eps_t[:], func=ACT.Abs_reciprocal_sqrt)
+
+        ident = const.tile([P, P], F32)
+        make_identity(nc, ident[:])
+
+        w_pairs = w_sb[:].bitcast(F32).rearrange("p (a g q u) -> p a g q u", a=O_STRIPES, g=PASSES, q=P, u=PAIRS)
+        w_grouped = const.tile([P, PASSES * OUT_CH * PACK], BF16, align_bytes=64)
+        w_grouped_pairs = w_grouped[:].bitcast(F32).rearrange("p (g o u) -> p g o u", g=PASSES, o=OUT_CH, u=PAIRS)
+        w_signed = const.tile([P, PASSES * OUT_CH * PACK], BF16, align_bytes=64)
+        w_codes = const.tile([P, PASSES, OUT_CH], U32, align_bytes=64)
+        w_scales = const.tile([P, PASSES, OUT_CH], U8, align_bytes=64)
+        for g in range(PASSES):
+            for a in range(O_STRIPES):
+                wt = z_pool.tile([P, PAIRS, P], F32, tag="z", name="wt")
+                for u in range(PAIRS):
+                    nc.tensor.transpose(wt[:, u, :], w_pairs[:, a, g, :, u], ident[:])
+                nc.vector.tensor_copy(
+                    out=w_grouped_pairs[:, g, a * P : (a + 1) * P, :], in_=wt[:].rearrange("p u o -> p o u")
+                )
+
+        def spread(bank, factor, first_col):
+            nc.tensor.matmul(out=bank[:], lhsT=factor[:], rhs=rows[:, first_col : first_col + BANK], start=True, stop=True)
+
+        alpha_t = const.tile([P, 1], F32)
+        sign = const.tile([P, 1], F32)
+        bias_bank = setup_pool.tile([P, BANK], F32, tag="setup")
+        spread(bias_bank, ones, ROW_BIAS)
+        nc.vector.tensor_copy(out=alpha_t[:], in_=bias_bank[:, ROW_ALPHA : ROW_ALPHA + 1])
+        nc.vector.tensor_scalar(out=sign[:], in0=alpha_t[:], scalar1=1.0, scalar2=2.0, op0=ALU.is_le, op1=ALU.mult)
+        nc.vector.tensor_scalar(out=sign[:], in0=sign[:], scalar1=-1.0, scalar2=None, op0=ALU.add)
+        signed_ones = const.tile([P, P], BF16)
+        nc.vector.tensor_scalar(out=signed_ones[:], in0=ones[:], scalar1=sign[:, 0:1], scalar2=None, op0=ALU.mult)
+        bias_cols_bank = setup_pool.tile([P, BANK], F32, tag="setup")
+        for a in range(O_STRIPES):
+            nc.tensor.matmul(
+                out=bias_cols_bank[:, a : a + 1],
+                lhsT=rows[:, ROW_BIAS + a * P : ROW_BIAS + (a + 1) * P],
+                rhs=signed_ones[:, 0:1],
+                start=True,
+                stop=True,
+            )
+
+        grouped = {}
+        x_codes = {}
+        x_scales = {}
+        z_banks = {}
+        slopes = {}
+        p_tiles = {}
+        pt_banks = {}
+        sums = {}
+        n_tiles = {}
+        neg_means = {}
+        squares = {}
+        totals_sq = {}
+        rstds = {}
+        gamma_t = const.tile([P, COLS], F32)
+        beta_t = const.tile([P, COLS], F32)
+
+        def copy_on_gpsimd(out, in_):
+            nc.gpsimd.tensor_scalar(out=out, in0=in_, scalar1=1.0, scalar2=0.0, op0=ALU.mult, op1=ALU.add)
+
+        def regroup(i, g, copy, first_step=0, end_step=P):
+            b, tt = divmod(i, T_STRIPES)
+            if (i, g) not in grouped:
+                pool = grouped_pool if g == 0 else grouped_late_pool
+                side = pool.tile([P, FREQ, P, PACK], BF16, tag="grouped", name="side", align_bytes=64)
+                grouped[(i, g)] = side
+            run = 1 if copy == copy_on_gpsimd else RUN
+            copy(
+                out=grouped[(i, g)][:, :, first_step:end_step, :].rearrange("p f (c i) j -> p f c j i", i=run),
+                in_=raw[(b, g)][:, :, :, tt * P + first_step : tt * P + end_step].rearrange(
+                    "p j f (c i) -> p f c j i", i=run
+                ),
+            )
+
+        def quantise(i, g):
+            if g == 0:
+                codes = code_pool.tile([P, PASSES, FREQ * P], U32, tag="codes", align_bytes=64)
+                scales = code_pool.tile([P, PASSES, FREQ * P], U8, tag="scales", align_bytes=64)
+                x_codes[i] = codes
+                x_scales[i] = scales
+            nc.vector.quantize_mx(
+                out=x_codes[i][:, g, :].bitcast(FP8X4),
+                scales=x_scales[i][:, g, :],
+                in_=grouped[(i, g)][:].rearrange("p f t j -> p (f t j)"),
+            )
+
+        def multiply(i, g):
+            for a in range(O_STRIPES):
+                if g == 0:
+                    z = z_pool.tile([P, BANK], F32, tag="z")
+                    z_banks[(i, a)] = z
+                nc.tensor.matmul_mx(
+                    out=z_banks[(i, a)][:],
+                    lhsT=w_codes[:, g, a * P : (a + 1) * P].bitcast(FP8X4),
+                    lhsT_scale=w_scales[:, g, a * P : (a + 1) * P],
+                    rhs=x_codes[i][:, g, :].bitcast(FP8X4),
+                    rhs_scale=x_scales[i][:, g, :],
+                    start=(g == 0),
+                    stop=(g == PASSES - 1),
+                )
+
+        def slope_branch(i, a):
+            if a == 0:
+                slope = slope_pool.tile([P, O_STRIPES, BANK], F32, tag="slope")
+                slopes[i] = slope
+            nc.scalar.activation(
+                out=slopes[i][:, a, :],
+                in_=z_banks[(i, a)][:],
+                func=ACT.Identity,
+                bias=slope_bias_col[:, a : a + 1],
+                scale=alpha_t[:, 0:1],
+            )
+
+        def prelu_and_turn(i):
+            p_tile = p_pool.tile([P, O_STRIPES, FREQ, P], F32, tag="p")
+            p_tiles[i] = p_tile
+            total = setup_pool.tile([P, BANK], F32, tag="setup", name="total")
+            sums[i] = total
+            for a in range(O_STRIPES):
+                nc.vector.scalar_tensor_tensor(
+                    out=p_tile[:, a, :, :].rearrange("p f t -> p (f t)"),
+                    in0=z_banks[(i, a)][:],
+                    scalar=bias_col[:, a : a + 1],
+                    in1=slopes[i][:, a, :],
+                    op0=ALU.add,
+                    op1=ALU.max,
+                )
+                pt = pt_pool.tile([P, FREQ, P], F32, tag="pt")
+                pt_banks[(i, a)] = pt
+                for f in range(FREQ):
+                    nc.tensor.transpose(pt[:, f, :], p_tile[:, a, f, :], ident[:])
+                for f in range(FREQ):
+                    nc.tensor.matmul(
+                        out=total[:, 0:P],
+                        lhsT=p_tile[:, a, f, :],
+                        rhs=ident[:],
+                        is_transpose=True,
+                        start=(a == 0 and f == 0),
+                        stop=(a == O_STRIPES - 1 and f == FREQ - 1),
+                    )
+
+        def mean(i):
+            neg_mean = small.tile([P, 1], F32, tag="neg_mean")
+            folded = square_pool.tile([P, P], F32, tag="folded")
+            nc.scalar.activation(out=folded[:], in_=sums[i][:, 0:P], func=ACT.Copy, scale=-1.0 / COLS, accum_out=neg_mean[:])
+            neg_means[i] = neg_mean
+
+        def deviation(i):
+            parts = small.tile([P, O_STRIPES], F32, tag="parts")
+            squares[i] = parts
+            for a in range(O_STRIPES):
+                square = square_pool.tile([P, BANK], BF16, tag="square")
+                nc.scalar.activation(
+                    out=square[:],
+                    in_=pt_banks[(i, a)][:].rearrange("p f o -> p (f o)"),
+                    func=ACT.Square,
+                    bias=neg_means[i][:, 0:1],
+                    scale=1.0,
+                    accum_out=parts[:, a : a + 1],
+                )
+
+        def add_squares(i):
+            total_sq = small.tile([P, 1], F32, tag="total_sq")
+            parts_copy = small.tile([P, O_STRIPES], F32, tag="parts_copy")
+            nc.scalar.activation(out=parts_copy[:], in_=squares[i][:], func=ACT.Copy, accum_out=total_sq[:])
+            totals_sq[i] = total_sq
+
+        def inverse_deviation(i):
+            rstd = small.tile([P, 1], F32, tag="rstd")
+            nc.scalar.activation(
+                out=rstd[:], in_=totals_sq[i][:], func=ACT.Abs_reciprocal_sqrt, bias=eps_t[:, 0:1], scale=1.0 / COLS
+            )
+            rstds[i] = rstd
+
+        def centre_and_gain(i):
+            n = n_pool.tile([P, COLS], F32, tag="n")
+            for a in range(O_STRIPES):
+                cols = slice(a * BANK, (a + 1) * BANK)
+                nc.vector.scalar_tensor_tensor(
+                    out=n[:, cols].rearrange("p (o f) -> p o f", f=FREQ),
+                    in0=pt_banks[(i, a)][:].rearrange("p f o -> p o f"),
+                    scalar=neg_means[i][:, 0:1],
+                    in1=gamma_t[:, cols].rearrange("p (o f) -> p o f", f=FREQ),
+                    op0=ALU.add,
+                    op1=ALU.mult,
+                )
+            n_tiles[i] = n
+
+        def scale_and_shift(i, first_head, end_head):
+            cols = slice(first_head * HEAD_COLS, end_head * HEAD_COLS)
+            n = n_tiles[i]
+            nc.vector.scalar_tensor_tensor(
+                out=n[:, cols], in0=n[:, cols], scalar=rstds[i][:, 0:1], in1=beta_t[:, cols], op0=ALU.mult, op1=ALU.add
+            )
+
+        def store(i, first_head, end_head):
+            b, tt = divmod(i, T_STRIPES)
+            heads = n_tiles[i][:].rearrange("p (h s d) -> p h s d", h=H, s=len(outs), d=HD)
+            for s, out in enumerate(outs):
+                nc.sync.dma_start(
+                    out=out[b, first_head:end_head, tt * P : (tt + 1) * P, :].rearrange("h t d -> t h d"),
+                    in_=heads[:, first_head:end_head, s, :],
+                )
+
+        regroup(0, 0, nc.scalar.copy)
+        regroup(0, 1, nc.scalar.copy)
+        nc.vector.tensor_scalar(out=w_signed[:], in0=w_grouped[:], scalar1=sign[:, 0:1], scalar2=None, op0=ALU.mult)
+        for g in range(PASSES):
+            for a in range(O_STRIPES):
+                first = (g * OUT_CH + a * P) * PACK
+                nc.vector.quantize_mx(
+                    out=w_codes[:, g, a * P : (a + 1) * P].bitcast(FP8X4),
+                    scales=w_scales[:, g, a * P : (a + 1) * P],
+                    in_=w_signed[:, first : first + P * PACK],
+                )
+        quantise(0, 0)
+        quantise(0, 1)
+        for k in range(BANKS):
+            gamma_bank = pt_pool.tile([P, BANK], F32, tag="pt", name="gamma_bank")
+            spread(gamma_bank, signed_ones, ROW_GAMMA + k * BANK)
+            nc.scalar.copy(out=gamma_t[:, k * BANK : (k + 1) * BANK], in_=gamma_bank[:])
+        for k in range(BANKS):
+            beta_bank = pt_pool.tile([P, BANK], F32, tag="pt", name="beta_bank")
+            spread(beta_bank, ones, ROW_BETA + k * BANK)
+            nc.scalar.copy(out=beta_t[:, k * BANK : (k + 1) * BANK], in_=beta_bank[:])
+        multiply(0, 0)
+        multiply(0, 1)
+        bias_col = const.tile([P, O_STRIPES], F32)
+        nc.vector.tensor_copy(out=bias_col[:], in_=bias_cols_bank[:, 0:O_STRIPES])
+        slope_bias_col = const.tile([P, O_STRIPES], F32)
+        nc.vector.tensor_scalar(out=slope_bias_col[:], in0=bias_col[:], scalar1=alpha_t[:, 0:1], scalar2=None, op0=ALU.mult)
+        regroup(1, 0, nc.vector.tensor_copy)
+        regroup(1, 1, nc.vector.tensor_copy)
+
+        for i in range(UNITS):
+            slope_branch(i, 0)
+            if i > 0:
+                add_squares(i - 1)
+            slope_branch(i, 1)
+            if i > 0:
+                inverse_deviation(i - 1)
+            slope_branch(i, 2)
+            prelu_and_turn(i)
+            if i + 2 < UNITS:
+                b_next, tt_next = divmod(i + 2, T_STRIPES)
+                if tt_next == 0 and b_next + 1 < B:
+                    new_x_tiles(b_next + 1)
+                    load_x(b_next + 1, slice(0, T))
+                regroup(i + 2, 0, nc.scalar.copy, 0, EARLY_STEPS)
+            if i + 1 < UNITS:
+                quantise(i + 1, 0)
+                multiply(i + 1, 0)
+                quantise(i + 1, 1)
+                multiply(i + 1, 1)
+            if i + 2 < UNITS:
+                regroup(i + 2, 1, copy_on_gpsimd)
+            if i > 0:
+                scale_and_shift(i - 1, 0, H)
+                store(i - 1, 0, H)
+            mean(i)
+            if i + 2 < UNITS:
+                regroup(i + 2, 0, nc.scalar.copy, EARLY_STEPS, P)
+            deviation(i)
+            centre_and_gain(i)
+        add_squares(UNITS - 1)
+        inverse_deviation(UNITS - 1)
+        for piece in range(LAST_PIECES):
+            first_head = piece * H // LAST_PIECES
+            end_head = (piece + 1) * H // LAST_PIECES
+            scale_and_shift(UNITS - 1, first_head, end_head)
+            store(UNITS - 1, first_head, end_head)

@@ -61,7 +61,8 @@ def tile_unified2dattentiononframe_pa_t_kernel(
         square_pool = ctx.enter_context(tc.tile_pool(name="square", bufs=2))
         z_pool = ctx.enter_context(tc.psum_pool(name="z", bufs=BANKS))
         pt_pool = ctx.enter_context(tc.psum_pool(name="pt", bufs=BANKS))
-        setup_pool = ctx.enter_context(tc.psum_pool(name="setup", bufs=2))
+        setup_pool = ctx.enter_context(tc.psum_pool(name="setup", bufs=1))
+        warm_pool = ctx.enter_context(tc.psum_pool(name="warm", bufs=1))
         ctx.enter_context(tc.manual_schedule())
 
         raw = {}
@@ -133,7 +134,7 @@ def tile_unified2dattentiononframe_pa_t_kernel(
         nc.vector.tensor_scalar(out=sign[:], in0=sign[:], scalar1=-1.0, scalar2=None, op0=ALU.add)
         signed_ones = const.tile([P, P], BF16)
         nc.vector.tensor_scalar(out=signed_ones[:], in0=ones[:], scalar1=sign[:, 0:1], scalar2=None, op0=ALU.mult)
-        bias_cols_bank = setup_pool.tile([P, BANK], F32, tag="setup")
+        bias_cols_bank = warm_pool.tile([P, BANK], F32, tag="warm")
         for a in range(O_STRIPES):
             nc.tensor.matmul(
                 out=bias_cols_bank[:, a : a + 1],
@@ -202,6 +203,10 @@ def tile_unified2dattentiononframe_pa_t_kernel(
                     start=(g == 0),
                     stop=(g == PASSES - 1),
                 )
+
+        def keep_warm(tile_ap, count=1):
+            for k in range(count):
+                nc.tensor.matmul(out=warm_bank[:, k * P : (k + 1) * P], lhsT=ident[:], rhs=tile_ap, start=True, stop=True)
 
         def slope_branch(i, a):
             if a == 0:
@@ -278,6 +283,7 @@ def tile_unified2dattentiononframe_pa_t_kernel(
 
         def centre_and_gain(i):
             n = n_pool.tile([P, COLS], F32, tag="n")
+            n_tiles[i] = n
             for a in range(O_STRIPES):
                 cols = slice(a * BANK, (a + 1) * BANK)
                 nc.vector.scalar_tensor_tensor(
@@ -288,7 +294,7 @@ def tile_unified2dattentiononframe_pa_t_kernel(
                     op0=ALU.add,
                     op1=ALU.mult,
                 )
-            n_tiles[i] = n
+                keep_warm(n[:, a * BANK : a * BANK + P])
 
         def scale_and_shift(i, first_head, end_head):
             cols = slice(first_head * HEAD_COLS, end_head * HEAD_COLS)
@@ -336,8 +342,11 @@ def tile_unified2dattentiononframe_pa_t_kernel(
         regroup(1, 0, nc.vector.tensor_copy)
         regroup(1, 1, nc.vector.tensor_copy)
 
+        warm_bank = warm_pool.tile([P, BANK], F32, tag="warm", name="warm_bank")
+
         for i in range(UNITS):
             slope_branch(i, 0)
+            keep_warm(slopes[i][:, 0, 0:P])
             if i > 0:
                 add_squares(i - 1)
             slope_branch(i, 1)
@@ -360,6 +369,7 @@ def tile_unified2dattentiononframe_pa_t_kernel(
                 regroup(i + 2, 1, copy_on_gpsimd)
             if i > 0:
                 scale_and_shift(i - 1, 0, H)
+                keep_warm(n_tiles[i - 1][:, 0:P], 2)
                 store(i - 1, 0, H)
             mean(i)
             if i + 2 < UNITS:

@@ -38,9 +38,8 @@ FLOPS = 2 * OUT_CH * CIN * B * FREQ * T
 
 ROW_BIAS = 0
 ROW_ALPHA = OUT_CH
-ROW_GAMMA = BANK
-ROW_BETA = BANK + COLS
-ROW_COLS = BANK + 2 * COLS
+
+HEAD_WARM = 4
 
 
 def tile_unified2dattentiononframe_pa_t_kernel(
@@ -79,25 +78,27 @@ def tile_unified2dattentiononframe_pa_t_kernel(
                     in_=x[b, g * K_PASS : (g + 1) * K_PASS, :, t_range].rearrange("(p j) f t -> p j f t", j=PACK),
                 )
 
-        rows = const.tile([P, ROW_COLS], BF16)
-        nc.vector.memset(rows[:], 0.0)
+        rows = const.tile([P, BANK], BF16)
+        nc.gpsimd.memset(rows[:].bitcast(U32), 0)
+        beta_row = const.tile([P, COLS], BF16)
+        nc.gpsimd.memset(beta_row[:].bitcast(U32), 0)
         ones = const.tile([P, P], BF16)
         nc.vector.memset(ones[:], 1.0)
         eps_t = const.tile([P, 1], F32)
         nc.vector.memset(eps_t[:], EPS)
+        gamma_row = const.tile([P, COLS], BF16)
+        nc.vector.memset(gamma_row[:], 0.0)
         w_sb = const.tile([P, O_STRIPES * CIN], BF16)
-        nc.sync.dma_start(
-            out=w_sb[:].rearrange("p (a c) -> p a c", a=O_STRIPES),
-            in_=qkv_w.rearrange("(a p) c -> p a c", p=P),
-        )
-        new_x_tiles(0)
-        load_x(0, slice(0, P))
         nc.sync.dma_start(out=rows[0:1, ROW_ALPHA : ROW_ALPHA + 1], in_=qkv_alpha.rearrange("(r o) -> r o", r=1))
         nc.sync.dma_start(out=rows[0:1, ROW_BIAS : ROW_BIAS + OUT_CH], in_=qkv_b.rearrange("(r o) -> r o", r=1))
-        nc.sync.dma_start(out=rows[0:1, ROW_GAMMA : ROW_GAMMA + COLS], in_=qkv_gamma.rearrange("r o c f -> r (o c f)"))
-        nc.sync.dma_start(out=rows[0:1, ROW_BETA : ROW_BETA + COLS], in_=qkv_beta.rearrange("r o c f -> r (o c f)"))
-        for tt in range(1, T_STRIPES):
-            load_x(0, slice(tt * P, (tt + 1) * P))
+        for a in range(O_STRIPES):
+            nc.sync.dma_start(out=w_sb[:, a * CIN : (a + 1) * CIN], in_=qkv_w[a * P : (a + 1) * P, :])
+        nc.sync.dma_start(out=beta_row[0:1, :], in_=qkv_beta.rearrange("r o c f -> r (o c f)"))
+        nc.sync.dma_start(out=gamma_row[0:1, :], in_=qkv_gamma.rearrange("r o c f -> r (o c f)"))
+        new_x_tiles(0)
+        load_x(0, slice(0, P))
+        load_x(0, slice(P, 2 * P))
+        load_x(0, slice(2 * P, T))
         new_x_tiles(1)
         load_x(1, slice(0, T))
 
@@ -107,34 +108,74 @@ def tile_unified2dattentiononframe_pa_t_kernel(
         ident = const.tile([P, P], F32)
         make_identity(nc, ident[:])
 
+        warm_bank = warm_pool.tile([P, BANK], F32, tag="warm")
+
+        def keep_warm(tile_ap, count=1):
+            for k in range(count):
+                nc.tensor.matmul(out=warm_bank[:, k * P : (k + 1) * P], lhsT=ident[:], rhs=tile_ap, start=True, stop=True)
+
+        keep_warm(ident[:], HEAD_WARM)
+
         w_pairs = w_sb[:].bitcast(F32).rearrange("p (a g q u) -> p a g q u", a=O_STRIPES, g=PASSES, q=P, u=PAIRS)
         w_grouped = const.tile([P, PASSES * OUT_CH * PACK], BF16, align_bytes=64)
         w_grouped_pairs = w_grouped[:].bitcast(F32).rearrange("p (g o u) -> p g o u", g=PASSES, o=OUT_CH, u=PAIRS)
         w_signed = const.tile([P, PASSES * OUT_CH * PACK], BF16, align_bytes=64)
         w_codes = const.tile([P, PASSES, OUT_CH], U32, align_bytes=64)
         w_scales = const.tile([P, PASSES, OUT_CH], U8, align_bytes=64)
-        for g in range(PASSES):
-            for a in range(O_STRIPES):
-                wt = z_pool.tile([P, PAIRS, P], F32, tag="z", name="wt")
-                for u in range(PAIRS):
-                    nc.tensor.transpose(wt[:, u, :], w_pairs[:, a, g, :, u], ident[:])
-                nc.vector.tensor_copy(
-                    out=w_grouped_pairs[:, g, a * P : (a + 1) * P, :], in_=wt[:].rearrange("p u o -> p o u")
-                )
-
-        def spread(bank, factor, first_col):
-            nc.tensor.matmul(out=bank[:], lhsT=factor[:], rhs=rows[:, first_col : first_col + BANK], start=True, stop=True)
-
         alpha_t = const.tile([P, 1], F32)
         sign = const.tile([P, 1], F32)
-        bias_bank = setup_pool.tile([P, BANK], F32, tag="setup")
-        spread(bias_bank, ones, ROW_BIAS)
-        nc.vector.tensor_copy(out=alpha_t[:], in_=bias_bank[:, ROW_ALPHA : ROW_ALPHA + 1])
-        nc.vector.tensor_scalar(out=sign[:], in0=alpha_t[:], scalar1=1.0, scalar2=2.0, op0=ALU.is_le, op1=ALU.mult)
-        nc.vector.tensor_scalar(out=sign[:], in0=sign[:], scalar1=-1.0, scalar2=None, op0=ALU.add)
         signed_ones = const.tile([P, P], BF16)
-        nc.vector.tensor_scalar(out=signed_ones[:], in0=ones[:], scalar1=sign[:, 0:1], scalar2=None, op0=ALU.mult)
-        bias_cols_bank = warm_pool.tile([P, BANK], F32, tag="warm")
+        bias_col = const.tile([P, O_STRIPES], F32)
+        slope_bias_col = const.tile([P, O_STRIPES], F32)
+
+        def turn_weights(k):
+            a, g = divmod(k, PASSES)
+            wt = z_pool.tile([P, PAIRS, P], F32, tag="z", name="wt")
+            for u in range(PAIRS):
+                nc.tensor.transpose(wt[:, u, :], w_pairs[:, a, g, :, u], ident[:])
+            nc.vector.tensor_copy(
+                out=w_grouped_pairs[:, g, a * P : (a + 1) * P, :], in_=wt[:].rearrange("p u o -> p o u")
+            )
+
+        def sign_weights(k):
+            a, g = divmod(k, PASSES)
+            first = (g * OUT_CH + a * P) * PACK
+            block = slice(first, first + P * PACK)
+            nc.vector.tensor_scalar(
+                out=w_signed[:, block], in0=w_grouped[:, block], scalar1=sign[:, 0:1], scalar2=None, op0=ALU.mult
+            )
+
+        def quantise_weights(k):
+            a, g = divmod(k, PASSES)
+            first = (g * OUT_CH + a * P) * PACK
+            nc.vector.quantize_mx(
+                out=w_codes[:, g, a * P : (a + 1) * P].bitcast(FP8X4),
+                scales=w_scales[:, g, a * P : (a + 1) * P],
+                in_=w_signed[:, first : first + P * PACK],
+            )
+
+        def spread(out, factor, row):
+            nc.tensor.matmul(out=out, lhsT=factor[:], rhs=row, start=True, stop=True)
+
+        def find_sign():
+            bias_bank = setup_pool.tile([P, BANK], F32, tag="setup")
+            spread(bias_bank[:], ones, rows[:])
+            nc.vector.tensor_copy(out=alpha_t[:], in_=bias_bank[:, ROW_ALPHA : ROW_ALPHA + 1])
+            nc.vector.tensor_scalar(out=sign[:], in0=alpha_t[:], scalar1=1.0, scalar2=2.0, op0=ALU.is_le, op1=ALU.mult)
+            nc.vector.tensor_scalar(out=sign[:], in0=sign[:], scalar1=-1.0, scalar2=None, op0=ALU.add)
+            nc.vector.tensor_scalar(out=signed_ones[:], in0=ones[:], scalar1=sign[:, 0:1], scalar2=None, op0=ALU.mult)
+
+        turn_weights(0)
+        turn_weights(1)
+        find_sign()
+        blocks = O_STRIPES * PASSES
+        for k in range(2, blocks + 2):
+            if k < blocks:
+                turn_weights(k)
+            sign_weights(k - 2)
+            if k > 2:
+                quantise_weights(k - 3)
+        bias_cols_bank = setup_pool.tile([P, BANK], F32, tag="setup")
         for a in range(O_STRIPES):
             nc.tensor.matmul(
                 out=bias_cols_bank[:, a : a + 1],
@@ -143,6 +184,33 @@ def tile_unified2dattentiononframe_pa_t_kernel(
                 start=True,
                 stop=True,
             )
+        nc.vector.tensor_copy(out=bias_col[:], in_=bias_cols_bank[:, 0:O_STRIPES])
+        quantise_weights(blocks - 1)
+        nc.vector.tensor_scalar(out=slope_bias_col[:], in0=bias_col[:], scalar1=alpha_t[:, 0:1], scalar2=None, op0=ALU.mult)
+
+        table = const.tile([P, 2 * COLS], BF16)
+        beta_t = table[:, 0:COLS]
+        gamma_t = table[:, COLS : 2 * COLS]
+        table_banks = []
+        for k in range(BANKS):
+            bank = pt_pool.tile([P, 2, BANK], BF16, tag="pt", name="bank")
+            for side in range(2):
+                piece = 2 * k + side
+                if piece < BANKS:
+                    spread(bank[:, side, :], ones, beta_row[:, piece * BANK : (piece + 1) * BANK])
+                else:
+                    spread(bank[:, side, :], signed_ones, gamma_row[:, (piece - BANKS) * BANK : (piece - BANKS + 1) * BANK])
+            table_banks.append(bank)
+
+        def copy_table(copy, first_piece, end_piece):
+            for k in range(BANKS):
+                first = max(first_piece, 2 * k)
+                end = min(end_piece, 2 * k + 2)
+                if first < end:
+                    copy(
+                        out=table[:, first * BANK : end * BANK],
+                        in_=table_banks[k][:, first - 2 * k : end - 2 * k, :].rearrange("p s c -> p (s c)"),
+                    )
 
         grouped = {}
         x_codes = {}
@@ -157,8 +225,6 @@ def tile_unified2dattentiononframe_pa_t_kernel(
         squares = {}
         totals_sq = {}
         rstds = {}
-        gamma_t = const.tile([P, COLS], F32)
-        beta_t = const.tile([P, COLS], F32)
 
         def copy_on_gpsimd(out, in_):
             nc.gpsimd.tensor_scalar(out=out, in0=in_, scalar1=1.0, scalar2=0.0, op0=ALU.mult, op1=ALU.add)
@@ -203,10 +269,6 @@ def tile_unified2dattentiononframe_pa_t_kernel(
                     start=(g == 0),
                     stop=(g == PASSES - 1),
                 )
-
-        def keep_warm(tile_ap, count=1):
-            for k in range(count):
-                nc.tensor.matmul(out=warm_bank[:, k * P : (k + 1) * P], lhsT=ident[:], rhs=tile_ap, start=True, stop=True)
 
         def slope_branch(i, a):
             if a == 0:
@@ -312,37 +374,18 @@ def tile_unified2dattentiononframe_pa_t_kernel(
                     in_=heads[:, first_head:end_head, s, :],
                 )
 
-        regroup(0, 0, nc.scalar.copy)
-        regroup(0, 1, nc.scalar.copy)
-        nc.vector.tensor_scalar(out=w_signed[:], in0=w_grouped[:], scalar1=sign[:, 0:1], scalar2=None, op0=ALU.mult)
-        for g in range(PASSES):
-            for a in range(O_STRIPES):
-                first = (g * OUT_CH + a * P) * PACK
-                nc.vector.quantize_mx(
-                    out=w_codes[:, g, a * P : (a + 1) * P].bitcast(FP8X4),
-                    scales=w_scales[:, g, a * P : (a + 1) * P],
-                    in_=w_signed[:, first : first + P * PACK],
-                )
+        half = P // 2
+        regroup(0, 0, nc.scalar.copy, 0, half)
+        regroup(0, 0, copy_on_gpsimd, half, P)
+        regroup(0, 1, nc.scalar.copy, 0, half)
+        regroup(0, 1, copy_on_gpsimd, half, P)
+        copy_table(nc.scalar.copy, 0, BANKS)
         quantise(0, 0)
-        quantise(0, 1)
-        for k in range(BANKS):
-            gamma_bank = pt_pool.tile([P, BANK], F32, tag="pt", name="gamma_bank")
-            spread(gamma_bank, signed_ones, ROW_GAMMA + k * BANK)
-            nc.scalar.copy(out=gamma_t[:, k * BANK : (k + 1) * BANK], in_=gamma_bank[:])
-        for k in range(BANKS):
-            beta_bank = pt_pool.tile([P, BANK], F32, tag="pt", name="beta_bank")
-            spread(beta_bank, ones, ROW_BETA + k * BANK)
-            nc.scalar.copy(out=beta_t[:, k * BANK : (k + 1) * BANK], in_=beta_bank[:])
         multiply(0, 0)
+        quantise(0, 1)
         multiply(0, 1)
-        bias_col = const.tile([P, O_STRIPES], F32)
-        nc.vector.tensor_copy(out=bias_col[:], in_=bias_cols_bank[:, 0:O_STRIPES])
-        slope_bias_col = const.tile([P, O_STRIPES], F32)
-        nc.vector.tensor_scalar(out=slope_bias_col[:], in0=bias_col[:], scalar1=alpha_t[:, 0:1], scalar2=None, op0=ALU.mult)
-        regroup(1, 0, nc.vector.tensor_copy)
-        regroup(1, 1, nc.vector.tensor_copy)
-
-        warm_bank = warm_pool.tile([P, BANK], F32, tag="warm", name="warm_bank")
+        copy_table(nc.vector.tensor_copy, BANKS, 2 * BANKS)
+        regroup(1, 1, copy_on_gpsimd)
 
         for i in range(UNITS):
             slope_branch(i, 0)
@@ -360,6 +403,8 @@ def tile_unified2dattentiononframe_pa_t_kernel(
                     new_x_tiles(b_next + 1)
                     load_x(b_next + 1, slice(0, T))
                 regroup(i + 2, 0, nc.scalar.copy, 0, EARLY_STEPS)
+            if i == 0:
+                regroup(1, 0, nc.vector.tensor_copy)
             if i + 1 < UNITS:
                 quantise(i + 1, 0)
                 multiply(i + 1, 0)

@@ -31,7 +31,9 @@ HEAD_COLS = COLS // H
 
 LAST_PIECES = 4
 
-EARLY_STEPS = 96
+FIRST_SCALAR_STEPS = 48
+SCALAR_STEPS = 64
+VECTOR_BINS = 0
 RUN = 4
 
 FLOPS = 2 * OUT_CH * CIN * B * FREQ * T
@@ -55,13 +57,12 @@ def tile_unified2dattentiononframe_pa_t_kernel(
         code_pool = ctx.enter_context(tc.tile_pool(name="codes", bufs=3))
         slope_pool = ctx.enter_context(tc.tile_pool(name="slope", bufs=2))
         p_pool = ctx.enter_context(tc.tile_pool(name="p", bufs=2))
-        n_pool = ctx.enter_context(tc.tile_pool(name="n", bufs=4))
+        n_pool = ctx.enter_context(tc.tile_pool(name="n", bufs=8))
         small = ctx.enter_context(tc.tile_pool(name="small", bufs=4))
         square_pool = ctx.enter_context(tc.tile_pool(name="square", bufs=2))
         z_pool = ctx.enter_context(tc.psum_pool(name="z", bufs=BANKS))
         pt_pool = ctx.enter_context(tc.psum_pool(name="pt", bufs=BANKS))
-        setup_pool = ctx.enter_context(tc.psum_pool(name="setup", bufs=1))
-        warm_pool = ctx.enter_context(tc.psum_pool(name="warm", bufs=1))
+        keep_pool = ctx.enter_context(tc.psum_pool(name="keep", bufs=1))
         ctx.enter_context(tc.manual_schedule())
 
         raw = {}
@@ -96,11 +97,11 @@ def tile_unified2dattentiononframe_pa_t_kernel(
         nc.sync.dma_start(out=beta_row[0:1, :], in_=qkv_beta.rearrange("r o c f -> r (o c f)"))
         nc.sync.dma_start(out=gamma_row[0:1, :], in_=qkv_gamma.rearrange("r o c f -> r (o c f)"))
         new_x_tiles(0)
-        load_x(0, slice(0, P))
-        load_x(0, slice(P, 2 * P))
-        load_x(0, slice(2 * P, T))
+        for tt in range(T_STRIPES):
+            load_x(0, slice(tt * P, (tt + 1) * P))
         new_x_tiles(1)
-        load_x(1, slice(0, T))
+        for half in range(2):
+            load_x(1, slice(half * T // 2, (half + 1) * T // 2))
 
         warm = const.tile([P, 1], F32)
         nc.scalar.activation(out=warm[:], in_=eps_t[:], func=ACT.Abs_reciprocal_sqrt)
@@ -108,11 +109,15 @@ def tile_unified2dattentiononframe_pa_t_kernel(
         ident = const.tile([P, P], F32)
         make_identity(nc, ident[:])
 
-        warm_bank = warm_pool.tile([P, BANK], F32, tag="warm")
+        beta_bank = keep_pool.tile([P, 2, BANK], BF16, tag="beta_bank")
+        mixed_bank = keep_pool.tile([P, BANK], F32, tag="mixed_bank")
+        beta_end = mixed_bank[:, 0 : BANK // 2].bitcast(BF16)
+        total = mixed_bank[:, BANK // 2 : BANK // 2 + P]
+        unread = mixed_bank[:, BANK // 2 + P : BANK]
 
         def keep_warm(tile_ap, count=1):
             for k in range(count):
-                nc.tensor.matmul(out=warm_bank[:, k * P : (k + 1) * P], lhsT=ident[:], rhs=tile_ap, start=True, stop=True)
+                nc.tensor.matmul(out=unread, lhsT=ident[:], rhs=tile_ap, start=True, stop=True)
 
         keep_warm(ident[:], HEAD_WARM)
 
@@ -127,6 +132,8 @@ def tile_unified2dattentiononframe_pa_t_kernel(
         signed_ones = const.tile([P, P], BF16)
         bias_col = const.tile([P, O_STRIPES], F32)
         slope_bias_col = const.tile([P, O_STRIPES], F32)
+        rest_t = const.tile([P, 1], F32)
+        rest_bias_col = const.tile([P, O_STRIPES], F32)
 
         def turn_weights(k):
             a, g = divmod(k, PASSES)
@@ -158,12 +165,15 @@ def tile_unified2dattentiononframe_pa_t_kernel(
             nc.tensor.matmul(out=out, lhsT=factor[:], rhs=row, start=True, stop=True)
 
         def find_sign():
-            bias_bank = setup_pool.tile([P, BANK], F32, tag="setup")
+            bias_bank = pt_pool.tile([P, BANK], F32, tag="pt")
             spread(bias_bank[:], ones, rows[:])
-            nc.vector.tensor_copy(out=alpha_t[:], in_=bias_bank[:, ROW_ALPHA : ROW_ALPHA + 1])
-            nc.vector.tensor_scalar(out=sign[:], in0=alpha_t[:], scalar1=1.0, scalar2=2.0, op0=ALU.is_le, op1=ALU.mult)
-            nc.vector.tensor_scalar(out=sign[:], in0=sign[:], scalar1=-1.0, scalar2=None, op0=ALU.add)
-            nc.vector.tensor_scalar(out=signed_ones[:], in0=ones[:], scalar1=sign[:, 0:1], scalar2=None, op0=ALU.mult)
+            nc.scalar.copy(out=alpha_t[:], in_=bias_bank[:, ROW_ALPHA : ROW_ALPHA + 1])
+            nc.gpsimd.tensor_scalar(out=sign[:], in0=alpha_t[:], scalar1=1.0, scalar2=2.0, op0=ALU.is_le, op1=ALU.mult)
+            nc.gpsimd.tensor_scalar(out=sign[:], in0=sign[:], scalar1=1.0, scalar2=-1.0, op0=ALU.mult, op1=ALU.add)
+            nc.gpsimd.tensor_scalar(
+                out=signed_ones[:], in0=ones[:], scalar1=sign[:, 0:1], scalar2=0.0, op0=ALU.mult, op1=ALU.add
+            )
+            nc.gpsimd.tensor_scalar(out=rest_t[:], in0=alpha_t[:], scalar1=-1.0, scalar2=1.0, op0=ALU.mult, op1=ALU.add)
 
         turn_weights(0)
         turn_weights(1)
@@ -175,7 +185,7 @@ def tile_unified2dattentiononframe_pa_t_kernel(
             sign_weights(k - 2)
             if k > 2:
                 quantise_weights(k - 3)
-        bias_cols_bank = setup_pool.tile([P, BANK], F32, tag="setup")
+        bias_cols_bank = pt_pool.tile([P, BANK], F32, tag="pt")
         for a in range(O_STRIPES):
             nc.tensor.matmul(
                 out=bias_cols_bank[:, a : a + 1],
@@ -184,33 +194,25 @@ def tile_unified2dattentiononframe_pa_t_kernel(
                 start=True,
                 stop=True,
             )
-        nc.vector.tensor_copy(out=bias_col[:], in_=bias_cols_bank[:, 0:O_STRIPES])
+        nc.scalar.copy(out=bias_col[:], in_=bias_cols_bank[:, 0:O_STRIPES])
         quantise_weights(blocks - 1)
-        nc.vector.tensor_scalar(out=slope_bias_col[:], in0=bias_col[:], scalar1=alpha_t[:, 0:1], scalar2=None, op0=ALU.mult)
+        for out, factor in ((slope_bias_col, alpha_t), (rest_bias_col, rest_t)):
+            nc.gpsimd.tensor_scalar(out=out[:], in0=bias_col[:], scalar1=factor[:, 0:1], scalar2=0.0, op0=ALU.mult, op1=ALU.add)
 
-        table = const.tile([P, 2 * COLS], BF16)
-        beta_t = table[:, 0:COLS]
-        gamma_t = table[:, COLS : 2 * COLS]
-        table_banks = []
         for k in range(BANKS):
-            bank = pt_pool.tile([P, 2, BANK], BF16, tag="pt", name="bank")
-            for side in range(2):
-                piece = 2 * k + side
-                if piece < BANKS:
-                    spread(bank[:, side, :], ones, beta_row[:, piece * BANK : (piece + 1) * BANK])
-                else:
-                    spread(bank[:, side, :], signed_ones, gamma_row[:, (piece - BANKS) * BANK : (piece - BANKS + 1) * BANK])
-            table_banks.append(bank)
+            spread(beta_bank[:, k, :] if k < 2 else beta_end, ones, beta_row[:, k * BANK : (k + 1) * BANK])
+        gamma_t = const.tile([P, COLS], BF16)
+        gamma_banks = []
+        for first in range(0, BANKS, 2):
+            gamma_bank = pt_pool.tile([P, 2, BANK], BF16, tag="pt")
+            for k in range(first, min(first + 2, BANKS)):
+                spread(gamma_bank[:, k - first, :], signed_ones, gamma_row[:, k * BANK : (k + 1) * BANK])
+            gamma_banks.append(gamma_bank)
 
-        def copy_table(copy, first_piece, end_piece):
-            for k in range(BANKS):
-                first = max(first_piece, 2 * k)
-                end = min(end_piece, 2 * k + 2)
-                if first < end:
-                    copy(
-                        out=table[:, first * BANK : end * BANK],
-                        in_=table_banks[k][:, first - 2 * k : end - 2 * k, :].rearrange("p s c -> p (s c)"),
-                    )
+        def copy_gamma(copy):
+            for k, bank in enumerate(gamma_banks):
+                cols = slice(2 * k * BANK, min(2 * (k + 1) * BANK, COLS))
+                copy(out=gamma_t[:, cols], in_=bank[:].rearrange("p s c -> p (s c)")[:, 0 : cols.stop - cols.start])
 
         grouped = {}
         x_codes = {}
@@ -219,7 +221,6 @@ def tile_unified2dattentiononframe_pa_t_kernel(
         slopes = {}
         p_tiles = {}
         pt_banks = {}
-        sums = {}
         n_tiles = {}
         neg_means = {}
         squares = {}
@@ -274,6 +275,8 @@ def tile_unified2dattentiononframe_pa_t_kernel(
             if a == 0:
                 slope = slope_pool.tile([P, O_STRIPES, BANK], F32, tag="slope")
                 slopes[i] = slope
+                p_tile = p_pool.tile([P, O_STRIPES, FREQ, P], F32, tag="p")
+                p_tiles[i] = p_tile
             nc.scalar.activation(
                 out=slopes[i][:, a, :],
                 in_=z_banks[(i, a)][:],
@@ -282,38 +285,60 @@ def tile_unified2dattentiononframe_pa_t_kernel(
                 scale=alpha_t[:, 0:1],
             )
 
-        def prelu_and_turn(i):
-            p_tile = p_pool.tile([P, O_STRIPES, FREQ, P], F32, tag="p")
-            p_tiles[i] = p_tile
-            total = setup_pool.tile([P, BANK], F32, tag="setup", name="total")
-            sums[i] = total
-            for a in range(O_STRIPES):
-                nc.vector.scalar_tensor_tensor(
-                    out=p_tile[:, a, :, :].rearrange("p f t -> p (f t)"),
-                    in0=z_banks[(i, a)][:],
-                    scalar=bias_col[:, a : a + 1],
-                    in1=slopes[i][:, a, :],
-                    op0=ALU.add,
-                    op1=ALU.max,
-                )
-                pt = pt_pool.tile([P, FREQ, P], F32, tag="pt")
-                pt_banks[(i, a)] = pt
-                for f in range(FREQ):
-                    nc.tensor.transpose(pt[:, f, :], p_tile[:, a, f, :], ident[:])
-                for f in range(FREQ):
+        def vector_bins(a):
+            return FREQ if a < O_STRIPES - 1 else VECTOR_BINS
+
+        def rest_branch(i, a):
+            nc.scalar.activation(
+                out=p_tiles[i][:, a, vector_bins(a) :, :].rearrange("p f t -> p (f t)"),
+                in_=z_banks[(i, a)][:, vector_bins(a) * P :],
+                func=ACT.Relu,
+                bias=rest_bias_col[:, a : a + 1],
+                scale=rest_t[:, 0:1],
+            )
+
+        def prelu(i, a):
+            nc.vector.scalar_tensor_tensor(
+                out=p_tiles[i][:, a, 0 : vector_bins(a), :].rearrange("p f t -> p (f t)"),
+                in0=z_banks[(i, a)][:, 0 : vector_bins(a) * P],
+                scalar=bias_col[:, a : a + 1],
+                in1=slopes[i][:, a, 0 : vector_bins(a) * P],
+                op0=ALU.add,
+                op1=ALU.max,
+            )
+
+        def turn(i, a):
+            pt = pt_pool.tile([P, FREQ, P], F32, tag="pt")
+            pt_banks[(i, a)] = pt
+            def parts(f):
+                one = p_tiles[i][:, a, f, :]
+                return [one] if f < vector_bins(a) else [one, slopes[i][:, a, f * P : (f + 1) * P]]
+
+            for f in range(FREQ):
+                for k, part in enumerate(parts(f)):
                     nc.tensor.matmul(
-                        out=total[:, 0:P],
-                        lhsT=p_tile[:, a, f, :],
+                        out=total,
+                        lhsT=part,
                         rhs=ident[:],
                         is_transpose=True,
-                        start=(a == 0 and f == 0),
-                        stop=(a == O_STRIPES - 1 and f == FREQ - 1),
+                        start=(a == 0 and f == 0 and k == 0),
+                        stop=(a == O_STRIPES - 1 and f == FREQ - 1 and k == len(parts(f)) - 1),
+                    )
+            for f in range(FREQ):
+                for k, part in enumerate(parts(f)):
+                    nc.tensor.matmul(
+                        out=pt[:, f, :],
+                        lhsT=part,
+                        rhs=ident[:],
+                        is_transpose=True,
+                        start=(k == 0),
+                        stop=(k == len(parts(f)) - 1),
                     )
 
         def mean(i):
             neg_mean = small.tile([P, 1], F32, tag="neg_mean")
             folded = square_pool.tile([P, P], F32, tag="folded")
-            nc.scalar.activation(out=folded[:], in_=sums[i][:, 0:P], func=ACT.Copy, scale=-1.0 / COLS, accum_out=neg_mean[:])
+            nc.scalar.activation(out=folded[:], in_=total, func=ACT.Copy, scale=-1.0 / COLS, accum_out=neg_mean[:])
             neg_means[i] = neg_mean
 
         def deviation(i):
@@ -356,14 +381,23 @@ def tile_unified2dattentiononframe_pa_t_kernel(
                     op0=ALU.add,
                     op1=ALU.mult,
                 )
-                keep_warm(n[:, a * BANK : a * BANK + P])
+                if a != 1:
+                    keep_warm(n[:, a * BANK : a * BANK + P])
 
         def scale_and_shift(i, first_head, end_head):
-            cols = slice(first_head * HEAD_COLS, end_head * HEAD_COLS)
             n = n_tiles[i]
-            nc.vector.scalar_tensor_tensor(
-                out=n[:, cols], in0=n[:, cols], scalar=rstds[i][:, 0:1], in1=beta_t[:, cols], op0=ALU.mult, op1=ALU.add
-            )
+            for bank, first_col in ((beta_bank[:].rearrange("p s c -> p (s c)"), 0), (beta_end, 2 * BANK)):
+                first = max(first_head * HEAD_COLS, first_col)
+                end = min(end_head * HEAD_COLS, min(first_col + 2 * BANK, COLS))
+                if first < end:
+                    nc.vector.scalar_tensor_tensor(
+                        out=n[:, first:end],
+                        in0=n[:, first:end],
+                        scalar=rstds[i][:, 0:1],
+                        in1=bank[:, first - first_col : end - first_col],
+                        op0=ALU.mult,
+                        op1=ALU.add,
+                    )
 
         def store(i, first_head, end_head):
             b, tt = divmod(i, T_STRIPES)
@@ -377,15 +411,14 @@ def tile_unified2dattentiononframe_pa_t_kernel(
         half = P // 2
         regroup(0, 0, nc.scalar.copy, 0, half)
         regroup(0, 0, copy_on_gpsimd, half, P)
-        regroup(0, 1, nc.scalar.copy, 0, half)
-        regroup(0, 1, copy_on_gpsimd, half, P)
-        copy_table(nc.scalar.copy, 0, BANKS)
+        copy_gamma(nc.scalar.copy)
         quantise(0, 0)
         multiply(0, 0)
+        regroup(0, 1, nc.scalar.copy, 0, FIRST_SCALAR_STEPS)
+        regroup(0, 1, nc.vector.tensor_copy, FIRST_SCALAR_STEPS, P)
         quantise(0, 1)
         multiply(0, 1)
-        copy_table(nc.vector.tensor_copy, BANKS, 2 * BANKS)
-        regroup(1, 1, copy_on_gpsimd)
+        regroup(1, 0, copy_on_gpsimd)
 
         for i in range(UNITS):
             slope_branch(i, 0)
@@ -396,30 +429,40 @@ def tile_unified2dattentiononframe_pa_t_kernel(
             if i > 0:
                 inverse_deviation(i - 1)
             slope_branch(i, 2)
-            prelu_and_turn(i)
+            if VECTOR_BINS < FREQ:
+                rest_branch(i, 2)
+            for a in range(O_STRIPES):
+                if vector_bins(a) > 0:
+                    prelu(i, a)
+                turn(i, a)
             if i + 2 < UNITS:
                 b_next, tt_next = divmod(i + 2, T_STRIPES)
                 if tt_next == 0 and b_next + 1 < B:
                     new_x_tiles(b_next + 1)
                     load_x(b_next + 1, slice(0, T))
-                regroup(i + 2, 0, nc.scalar.copy, 0, EARLY_STEPS)
+                if i > 0:
+                    regroup(i + 2, 0, nc.scalar.copy, 0, SCALAR_STEPS)
             if i == 0:
-                regroup(1, 0, nc.vector.tensor_copy)
+                regroup(1, 1, nc.vector.tensor_copy)
             if i + 1 < UNITS:
                 quantise(i + 1, 0)
                 multiply(i + 1, 0)
                 quantise(i + 1, 1)
                 multiply(i + 1, 1)
             if i + 2 < UNITS:
+                if i == 0:
+                    regroup(2, 0, copy_on_gpsimd, SCALAR_STEPS, P)
                 regroup(i + 2, 1, copy_on_gpsimd)
+                if i > 0:
+                    regroup(i + 2, 0, copy_on_gpsimd, SCALAR_STEPS, P)
+            mean(i)
             if i > 0:
                 scale_and_shift(i - 1, 0, H)
-                keep_warm(n_tiles[i - 1][:, 0:P], 2)
+                keep_warm(n_tiles[i - 1][:, 0:P])
                 store(i - 1, 0, H)
-            mean(i)
-            if i + 2 < UNITS:
-                regroup(i + 2, 0, nc.scalar.copy, EARLY_STEPS, P)
             deviation(i)
+            if i == 0:
+                regroup(2, 0, nc.scalar.copy, 0, SCALAR_STEPS)
             centre_and_gain(i)
         add_squares(UNITS - 1)
         inverse_deviation(UNITS - 1)

@@ -32,8 +32,7 @@ HEAD_COLS = COLS // H
 LAST_PIECES = 4
 
 FIRST_SCALAR_STEPS = 48
-SCALAR_STEPS = 64
-VECTOR_BINS = 0
+SCALAR_STEPS = 96
 RUN = 4
 
 FLOPS = 2 * OUT_CH * CIN * B * FREQ * T
@@ -132,8 +131,6 @@ def tile_unified2dattentiononframe_pa_t_kernel(
         signed_ones = const.tile([P, P], BF16)
         bias_col = const.tile([P, O_STRIPES], F32)
         slope_bias_col = const.tile([P, O_STRIPES], F32)
-        rest_t = const.tile([P, 1], F32)
-        rest_bias_col = const.tile([P, O_STRIPES], F32)
 
         def turn_weights(k):
             a, g = divmod(k, PASSES)
@@ -173,7 +170,6 @@ def tile_unified2dattentiononframe_pa_t_kernel(
             nc.gpsimd.tensor_scalar(
                 out=signed_ones[:], in0=ones[:], scalar1=sign[:, 0:1], scalar2=0.0, op0=ALU.mult, op1=ALU.add
             )
-            nc.gpsimd.tensor_scalar(out=rest_t[:], in0=alpha_t[:], scalar1=-1.0, scalar2=1.0, op0=ALU.mult, op1=ALU.add)
 
         turn_weights(0)
         turn_weights(1)
@@ -196,8 +192,9 @@ def tile_unified2dattentiononframe_pa_t_kernel(
             )
         nc.scalar.copy(out=bias_col[:], in_=bias_cols_bank[:, 0:O_STRIPES])
         quantise_weights(blocks - 1)
-        for out, factor in ((slope_bias_col, alpha_t), (rest_bias_col, rest_t)):
-            nc.gpsimd.tensor_scalar(out=out[:], in0=bias_col[:], scalar1=factor[:, 0:1], scalar2=0.0, op0=ALU.mult, op1=ALU.add)
+        nc.gpsimd.tensor_scalar(
+            out=slope_bias_col[:], in0=bias_col[:], scalar1=alpha_t[:, 0:1], scalar2=0.0, op0=ALU.mult, op1=ALU.add
+        )
 
         for k in range(BANKS):
             spread(beta_bank[:, k, :] if k < 2 else beta_end, ones, beta_row[:, k * BANK : (k + 1) * BANK])
@@ -285,55 +282,28 @@ def tile_unified2dattentiononframe_pa_t_kernel(
                 scale=alpha_t[:, 0:1],
             )
 
-        def vector_bins(a):
-            return FREQ if a < O_STRIPES - 1 else VECTOR_BINS
-
-        def rest_branch(i, a):
-            nc.scalar.activation(
-                out=p_tiles[i][:, a, vector_bins(a) :, :].rearrange("p f t -> p (f t)"),
-                in_=z_banks[(i, a)][:, vector_bins(a) * P :],
-                func=ACT.Relu,
-                bias=rest_bias_col[:, a : a + 1],
-                scale=rest_t[:, 0:1],
-            )
-
-        def prelu(i, a):
+        def prelu_and_turn(i, a):
             nc.vector.scalar_tensor_tensor(
-                out=p_tiles[i][:, a, 0 : vector_bins(a), :].rearrange("p f t -> p (f t)"),
-                in0=z_banks[(i, a)][:, 0 : vector_bins(a) * P],
+                out=p_tiles[i][:, a, :, :].rearrange("p f t -> p (f t)"),
+                in0=z_banks[(i, a)][:],
                 scalar=bias_col[:, a : a + 1],
-                in1=slopes[i][:, a, 0 : vector_bins(a) * P],
+                in1=slopes[i][:, a, :],
                 op0=ALU.add,
                 op1=ALU.max,
             )
-
-        def turn(i, a):
+            for f in range(FREQ):
+                nc.tensor.matmul(
+                    out=total,
+                    lhsT=p_tiles[i][:, a, f, :],
+                    rhs=ident[:],
+                    is_transpose=True,
+                    start=(a == 0 and f == 0),
+                    stop=(a == O_STRIPES - 1 and f == FREQ - 1),
+                )
             pt = pt_pool.tile([P, FREQ, P], F32, tag="pt")
             pt_banks[(i, a)] = pt
-            def parts(f):
-                one = p_tiles[i][:, a, f, :]
-                return [one] if f < vector_bins(a) else [one, slopes[i][:, a, f * P : (f + 1) * P]]
-
             for f in range(FREQ):
-                for k, part in enumerate(parts(f)):
-                    nc.tensor.matmul(
-                        out=total,
-                        lhsT=part,
-                        rhs=ident[:],
-                        is_transpose=True,
-                        start=(a == 0 and f == 0 and k == 0),
-                        stop=(a == O_STRIPES - 1 and f == FREQ - 1 and k == len(parts(f)) - 1),
-                    )
-            for f in range(FREQ):
-                for k, part in enumerate(parts(f)):
-                    nc.tensor.matmul(
-                        out=pt[:, f, :],
-                        lhsT=part,
-                        rhs=ident[:],
-                        is_transpose=True,
-                        start=(k == 0),
-                        stop=(k == len(parts(f)) - 1),
-                    )
+                nc.tensor.transpose(pt[:, f, :], p_tiles[i][:, a, f, :], ident[:])
 
         def mean(i):
             neg_mean = small.tile([P, 1], F32, tag="neg_mean")
@@ -429,12 +399,8 @@ def tile_unified2dattentiononframe_pa_t_kernel(
             if i > 0:
                 inverse_deviation(i - 1)
             slope_branch(i, 2)
-            if VECTOR_BINS < FREQ:
-                rest_branch(i, 2)
             for a in range(O_STRIPES):
-                if vector_bins(a) > 0:
-                    prelu(i, a)
-                turn(i, a)
+                prelu_and_turn(i, a)
             if i + 2 < UNITS:
                 b_next, tt_next = divmod(i + 2, T_STRIPES)
                 if tt_next == 0 and b_next + 1 < B:

@@ -109,16 +109,15 @@ def tile_unified2dattentiononframe_pa_t_kernel(
         make_identity(nc, ident[:])
 
         beta_bank = keep_pool.tile([P, 2, BANK], BF16, tag="beta_bank")
-        mixed_bank = keep_pool.tile([P, BANK], F32, tag="mixed_bank")
-        beta_end = mixed_bank[:, 0 : BANK // 2].bitcast(BF16)
-        total = mixed_bank[:, BANK // 2 : BANK // 2 + P]
-        unread = mixed_bank[:, BANK // 2 + P : BANK]
+        sums_bank = keep_pool.tile([P, FREQ, P], F32, tag="sums_bank")
+        total = sums_bank[:, 0, :]
+        unread = sums_bank[:, 1, :]
 
-        def keep_warm(tile_ap, count=1):
-            for k in range(count):
-                nc.tensor.matmul(out=unread, lhsT=ident[:], rhs=tile_ap, start=True, stop=True)
+        def keep_warm(out, tile_ap):
+            nc.tensor.matmul(out=out, lhsT=ident[:], rhs=tile_ap, start=True, stop=True)
 
-        keep_warm(ident[:], HEAD_WARM)
+        for k in range(HEAD_WARM):
+            keep_warm(unread, ident[:])
 
         w_pairs = w_sb[:].bitcast(F32).rearrange("p (a g q u) -> p a g q u", a=O_STRIPES, g=PASSES, q=P, u=PAIRS)
         w_grouped = const.tile([P, PASSES * OUT_CH * PACK], BF16, align_bytes=64)
@@ -196,20 +195,24 @@ def tile_unified2dattentiononframe_pa_t_kernel(
             out=slope_bias_col[:], in0=bias_col[:], scalar1=alpha_t[:, 0:1], scalar2=0.0, op0=ALU.mult, op1=ALU.add
         )
 
-        for k in range(BANKS):
-            spread(beta_bank[:, k, :] if k < 2 else beta_end, ones, beta_row[:, k * BANK : (k + 1) * BANK])
-        gamma_t = const.tile([P, COLS], BF16)
-        gamma_banks = []
-        for first in range(0, BANKS, 2):
-            gamma_bank = pt_pool.tile([P, 2, BANK], BF16, tag="pt")
-            for k in range(first, min(first + 2, BANKS)):
-                spread(gamma_bank[:, k - first, :], signed_ones, gamma_row[:, k * BANK : (k + 1) * BANK])
-            gamma_banks.append(gamma_bank)
+        for k in range(2):
+            spread(beta_bank[:, k, :], ones, beta_row[:, k * BANK : (k + 1) * BANK])
+        table = const.tile([P, 4, BANK], BF16)
+        gamma_t = table[:, 0:BANKS, :].rearrange("p k c -> p (k c)")
+        beta_end = table[:, BANKS, :]
+        table_banks = []
+        for first in range(0, 4, 2):
+            bank = pt_pool.tile([P, 2, BANK], BF16, tag="pt", name="bank")
+            for k in range(first, first + 2):
+                if k < BANKS:
+                    spread(bank[:, k - first, :], signed_ones, gamma_row[:, k * BANK : (k + 1) * BANK])
+                else:
+                    spread(bank[:, k - first, :], ones, beta_row[:, 2 * BANK : 3 * BANK])
+            table_banks.append(bank)
 
-        def copy_gamma(copy):
-            for k, bank in enumerate(gamma_banks):
-                cols = slice(2 * k * BANK, min(2 * (k + 1) * BANK, COLS))
-                copy(out=gamma_t[:, cols], in_=bank[:].rearrange("p s c -> p (s c)")[:, 0 : cols.stop - cols.start])
+        def copy_table(copy):
+            for k, bank in enumerate(table_banks):
+                copy(out=table[:, 2 * k : 2 * k + 2, :], in_=bank[:])
 
         grouped = {}
         x_codes = {}
@@ -300,10 +303,11 @@ def tile_unified2dattentiononframe_pa_t_kernel(
                     start=(a == 0 and f == 0),
                     stop=(a == O_STRIPES - 1 and f == FREQ - 1),
                 )
-            pt = pt_pool.tile([P, FREQ, P], F32, tag="pt")
-            pt_banks[(i, a)] = pt
+            pt = pt_banks[(i, a)]
             for f in range(FREQ):
                 nc.tensor.transpose(pt[:, f, :], p_tiles[i][:, a, f, :], ident[:])
+            if a < O_STRIPES - 1:
+                keep_warm(pt_banks[(i, a + 1)][:, 0, :], p_tiles[i][:, a, 0, :])
 
         def mean(i):
             neg_mean = small.tile([P, 1], F32, tag="neg_mean")
@@ -351,12 +355,12 @@ def tile_unified2dattentiononframe_pa_t_kernel(
                     op0=ALU.add,
                     op1=ALU.mult,
                 )
-                if a != 1:
-                    keep_warm(n[:, a * BANK : a * BANK + P])
+                if a < O_STRIPES - 1:
+                    keep_warm(unread, n[:, a * BANK : a * BANK + P])
 
         def scale_and_shift(i, first_head, end_head):
             n = n_tiles[i]
-            for bank, first_col in ((beta_bank[:].rearrange("p s c -> p (s c)"), 0), (beta_end, 2 * BANK)):
+            for bank, first_col in ((beta_end, 2 * BANK), (beta_bank[:].rearrange("p s c -> p (s c)"), 0)):
                 first = max(first_head * HEAD_COLS, first_col)
                 end = min(end_head * HEAD_COLS, min(first_col + 2 * BANK, COLS))
                 if first < end:
@@ -381,7 +385,7 @@ def tile_unified2dattentiononframe_pa_t_kernel(
         half = P // 2
         regroup(0, 0, nc.scalar.copy, 0, half)
         regroup(0, 0, copy_on_gpsimd, half, P)
-        copy_gamma(nc.scalar.copy)
+        copy_table(nc.scalar.copy)
         quantise(0, 0)
         multiply(0, 0)
         regroup(0, 1, nc.scalar.copy, 0, FIRST_SCALAR_STEPS)
@@ -392,13 +396,16 @@ def tile_unified2dattentiononframe_pa_t_kernel(
 
         for i in range(UNITS):
             slope_branch(i, 0)
-            keep_warm(slopes[i][:, 0, 0:P])
+            keep_warm(unread, slopes[i][:, 0, 0:P])
             if i > 0:
                 add_squares(i - 1)
             slope_branch(i, 1)
             if i > 0:
                 inverse_deviation(i - 1)
             slope_branch(i, 2)
+            for a in range(O_STRIPES):
+                pt = pt_pool.tile([P, FREQ, P], F32, tag="pt")
+                pt_banks[(i, a)] = pt
             for a in range(O_STRIPES):
                 prelu_and_turn(i, a)
             if i + 2 < UNITS:
@@ -424,7 +431,7 @@ def tile_unified2dattentiononframe_pa_t_kernel(
             mean(i)
             if i > 0:
                 scale_and_shift(i - 1, 0, H)
-                keep_warm(n_tiles[i - 1][:, 0:P])
+                keep_warm(unread, n_tiles[i - 1][:, 0:P])
                 store(i - 1, 0, H)
             deviation(i)
             if i == 0:

@@ -107,6 +107,8 @@ def tile_unified2dattentiononframe_pa_t_kernel(
 
         ident = const.tile([P, P], F32)
         make_identity(nc, ident[:])
+        warm_copy = const.tile([P, 1], F32)
+        nc.gpsimd.tensor_scalar(out=warm_copy[:], in0=ident[:, 0:1], scalar1=1.0, scalar2=0.0, op0=ALU.mult, op1=ALU.add)
 
         beta_bank = keep_pool.tile([P, 2, BANK], BF16, tag="beta_bank")
         sums_bank = keep_pool.tile([P, FREQ, P], F32, tag="sums_bank")
@@ -163,12 +165,10 @@ def tile_unified2dattentiononframe_pa_t_kernel(
         def find_sign():
             bias_bank = pt_pool.tile([P, BANK], F32, tag="pt")
             spread(bias_bank[:], ones, rows[:])
-            nc.scalar.copy(out=alpha_t[:], in_=bias_bank[:, ROW_ALPHA : ROW_ALPHA + 1])
-            nc.gpsimd.tensor_scalar(out=sign[:], in0=alpha_t[:], scalar1=1.0, scalar2=2.0, op0=ALU.is_le, op1=ALU.mult)
-            nc.gpsimd.tensor_scalar(out=sign[:], in0=sign[:], scalar1=1.0, scalar2=-1.0, op0=ALU.mult, op1=ALU.add)
-            nc.gpsimd.tensor_scalar(
-                out=signed_ones[:], in0=ones[:], scalar1=sign[:, 0:1], scalar2=0.0, op0=ALU.mult, op1=ALU.add
-            )
+            nc.vector.tensor_copy(out=alpha_t[:], in_=bias_bank[:, ROW_ALPHA : ROW_ALPHA + 1])
+            nc.vector.tensor_scalar(out=sign[:], in0=alpha_t[:], scalar1=1.0, scalar2=2.0, op0=ALU.is_le, op1=ALU.mult)
+            nc.vector.tensor_scalar(out=sign[:], in0=sign[:], scalar1=-1.0, scalar2=None, op0=ALU.add)
+            nc.vector.tensor_scalar(out=signed_ones[:], in0=ones[:], scalar1=sign[:, 0:1], scalar2=None, op0=ALU.mult)
 
         turn_weights(0)
         turn_weights(1)
@@ -189,11 +189,9 @@ def tile_unified2dattentiononframe_pa_t_kernel(
                 start=True,
                 stop=True,
             )
-        nc.scalar.copy(out=bias_col[:], in_=bias_cols_bank[:, 0:O_STRIPES])
+        nc.vector.tensor_copy(out=bias_col[:], in_=bias_cols_bank[:, 0:O_STRIPES])
         quantise_weights(blocks - 1)
-        nc.gpsimd.tensor_scalar(
-            out=slope_bias_col[:], in0=bias_col[:], scalar1=alpha_t[:, 0:1], scalar2=0.0, op0=ALU.mult, op1=ALU.add
-        )
+        nc.vector.tensor_scalar(out=slope_bias_col[:], in0=bias_col[:], scalar1=alpha_t[:, 0:1], scalar2=None, op0=ALU.mult)
 
         for k in range(2):
             spread(beta_bank[:, k, :], ones, beta_row[:, k * BANK : (k + 1) * BANK])
@@ -382,17 +380,16 @@ def tile_unified2dattentiononframe_pa_t_kernel(
                     in_=heads[:, first_head:end_head, s, :],
                 )
 
-        half = P // 2
-        regroup(0, 0, nc.scalar.copy, 0, half)
-        regroup(0, 0, copy_on_gpsimd, half, P)
-        copy_table(nc.scalar.copy)
+        regroup(0, 0, nc.scalar.copy)
         quantise(0, 0)
         multiply(0, 0)
         regroup(0, 1, nc.scalar.copy, 0, FIRST_SCALAR_STEPS)
         regroup(0, 1, nc.vector.tensor_copy, FIRST_SCALAR_STEPS, P)
+        copy_table(nc.scalar.copy)
         quantise(0, 1)
         multiply(0, 1)
-        regroup(1, 0, copy_on_gpsimd)
+        regroup(1, 0, nc.vector.tensor_copy)
+        regroup(1, 1, copy_on_gpsimd)
 
         for i in range(UNITS):
             slope_branch(i, 0)
@@ -415,19 +412,14 @@ def tile_unified2dattentiononframe_pa_t_kernel(
                     load_x(b_next + 1, slice(0, T))
                 if i > 0:
                     regroup(i + 2, 0, nc.scalar.copy, 0, SCALAR_STEPS)
-            if i == 0:
-                regroup(1, 1, nc.vector.tensor_copy)
             if i + 1 < UNITS:
                 quantise(i + 1, 0)
                 multiply(i + 1, 0)
                 quantise(i + 1, 1)
                 multiply(i + 1, 1)
             if i + 2 < UNITS:
-                if i == 0:
-                    regroup(2, 0, copy_on_gpsimd, SCALAR_STEPS, P)
                 regroup(i + 2, 1, copy_on_gpsimd)
-                if i > 0:
-                    regroup(i + 2, 0, copy_on_gpsimd, SCALAR_STEPS, P)
+                regroup(i + 2, 0, copy_on_gpsimd, SCALAR_STEPS, P)
             mean(i)
             if i > 0:
                 scale_and_shift(i - 1, 0, H)

@@ -32,7 +32,9 @@ HEAD_COLS = COLS // H
 LAST_PIECES = 4
 
 FIRST_SCALAR_STEPS = 48
-SCALAR_STEPS = 96
+SCALAR_STEPS = 80
+THIRD_SCALAR_STEPS = 48
+VECTOR_BINS = 2
 RUN = 4
 
 FLOPS = 2 * OUT_CH * CIN * B * FREQ * T
@@ -132,6 +134,8 @@ def tile_unified2dattentiononframe_pa_t_kernel(
         signed_ones = const.tile([P, P], BF16)
         bias_col = const.tile([P, O_STRIPES], F32)
         slope_bias_col = const.tile([P, O_STRIPES], F32)
+        rest_t = const.tile([P, 1], F32)
+        rest_bias_col = const.tile([P, O_STRIPES], F32)
 
         def turn_weights(k):
             a, g = divmod(k, PASSES)
@@ -191,7 +195,9 @@ def tile_unified2dattentiononframe_pa_t_kernel(
             )
         nc.vector.tensor_copy(out=bias_col[:], in_=bias_cols_bank[:, 0:O_STRIPES])
         quantise_weights(blocks - 1)
-        nc.vector.tensor_scalar(out=slope_bias_col[:], in0=bias_col[:], scalar1=alpha_t[:, 0:1], scalar2=None, op0=ALU.mult)
+        nc.vector.tensor_scalar(out=rest_t[:], in0=alpha_t[:], scalar1=-1.0, scalar2=1.0, op0=ALU.mult, op1=ALU.add)
+        for out, factor in ((slope_bias_col, alpha_t), (rest_bias_col, rest_t)):
+            nc.vector.tensor_scalar(out=out[:], in0=bias_col[:], scalar1=factor[:, 0:1], scalar2=None, op0=ALU.mult)
 
         for k in range(2):
             spread(beta_bank[:, k, :], ones, beta_row[:, k * BANK : (k + 1) * BANK])
@@ -283,29 +289,57 @@ def tile_unified2dattentiononframe_pa_t_kernel(
                 scale=alpha_t[:, 0:1],
             )
 
-        def prelu_and_turn(i, a):
+        def vector_bins(a):
+            return VECTOR_BINS if a == O_STRIPES - 1 else FREQ
+
+        def prelu(i, a):
+            bins = vector_bins(a)
             nc.vector.scalar_tensor_tensor(
-                out=p_tiles[i][:, a, :, :].rearrange("p f t -> p (f t)"),
-                in0=z_banks[(i, a)][:],
+                out=p_tiles[i][:, a, 0:bins, :].rearrange("p f t -> p (f t)"),
+                in0=z_banks[(i, a)][:, 0 : bins * P],
                 scalar=bias_col[:, a : a + 1],
-                in1=slopes[i][:, a, :],
+                in1=slopes[i][:, a, 0 : bins * P],
                 op0=ALU.add,
                 op1=ALU.max,
             )
+
+        def rest_branch(i, a):
+            bins = vector_bins(a)
+            nc.scalar.activation(
+                out=p_tiles[i][:, a, bins:FREQ, :].rearrange("p f t -> p (f t)"),
+                in_=z_banks[(i, a)][:, bins * P : FREQ * P],
+                func=ACT.Relu,
+                bias=rest_bias_col[:, a : a + 1],
+                scale=rest_t[:, 0:1],
+            )
+
+        def turn(i, a):
+            pieces = []
             for f in range(FREQ):
+                terms = [p_tiles[i][:, a, f, :]]
+                if f >= vector_bins(a):
+                    terms.append(slopes[i][:, a, f * P : (f + 1) * P])
+                pieces.append(terms)
+            flat = [term for terms in pieces for term in terms]
+            for k, term in enumerate(flat):
                 nc.tensor.matmul(
                     out=total,
-                    lhsT=p_tiles[i][:, a, f, :],
+                    lhsT=term,
                     rhs=ident[:],
                     is_transpose=True,
-                    start=(a == 0 and f == 0),
-                    stop=(a == O_STRIPES - 1 and f == FREQ - 1),
+                    start=(a == 0 and k == 0),
+                    stop=(a == O_STRIPES - 1 and k == len(flat) - 1),
                 )
-            pt = pt_banks[(i, a)]
-            for f in range(FREQ):
-                nc.tensor.transpose(pt[:, f, :], p_tiles[i][:, a, f, :], ident[:])
-            if a < O_STRIPES - 1:
-                keep_warm(pt_banks[(i, a + 1)][:, 0, :], p_tiles[i][:, a, 0, :])
+            for f, terms in enumerate(pieces):
+                for k, term in enumerate(terms):
+                    nc.tensor.matmul(
+                        out=pt_banks[(i, a)][:, f, :],
+                        lhsT=term,
+                        rhs=ident[:],
+                        is_transpose=True,
+                        start=(k == 0),
+                        stop=(k == len(terms) - 1),
+                    )
 
         def mean(i):
             neg_mean = small.tile([P, 1], F32, tag="neg_mean")
@@ -353,7 +387,7 @@ def tile_unified2dattentiononframe_pa_t_kernel(
                     op0=ALU.add,
                     op1=ALU.mult,
                 )
-                if a < O_STRIPES - 1:
+                if a != 1:
                     keep_warm(unread, n[:, a * BANK : a * BANK + P])
 
         def scale_and_shift(i, first_head, end_head):
@@ -389,7 +423,6 @@ def tile_unified2dattentiononframe_pa_t_kernel(
         quantise(0, 1)
         multiply(0, 1)
         regroup(1, 0, nc.vector.tensor_copy)
-        regroup(1, 1, copy_on_gpsimd)
 
         for i in range(UNITS):
             slope_branch(i, 0)
@@ -403,8 +436,10 @@ def tile_unified2dattentiononframe_pa_t_kernel(
             for a in range(O_STRIPES):
                 pt = pt_pool.tile([P, FREQ, P], F32, tag="pt")
                 pt_banks[(i, a)] = pt
+            rest_branch(i, O_STRIPES - 1)
             for a in range(O_STRIPES):
-                prelu_and_turn(i, a)
+                prelu(i, a)
+                turn(i, a)
             if i + 2 < UNITS:
                 b_next, tt_next = divmod(i + 2, T_STRIPES)
                 if tt_next == 0 and b_next + 1 < B:
@@ -412,14 +447,20 @@ def tile_unified2dattentiononframe_pa_t_kernel(
                     load_x(b_next + 1, slice(0, T))
                 if i > 0:
                     regroup(i + 2, 0, nc.scalar.copy, 0, SCALAR_STEPS)
+            if i == 0:
+                regroup(1, 1, nc.scalar.copy, 0, P // 2)
+                regroup(1, 1, nc.vector.tensor_copy, P // 2, P)
             if i + 1 < UNITS:
                 quantise(i + 1, 0)
                 multiply(i + 1, 0)
                 quantise(i + 1, 1)
                 multiply(i + 1, 1)
             if i + 2 < UNITS:
+                if i == 0:
+                    regroup(2, 0, copy_on_gpsimd, THIRD_SCALAR_STEPS, P)
                 regroup(i + 2, 1, copy_on_gpsimd)
-                regroup(i + 2, 0, copy_on_gpsimd, SCALAR_STEPS, P)
+                if i > 0:
+                    regroup(i + 2, 0, copy_on_gpsimd, SCALAR_STEPS, P)
             mean(i)
             if i > 0:
                 scale_and_shift(i - 1, 0, H)
@@ -427,7 +468,7 @@ def tile_unified2dattentiononframe_pa_t_kernel(
                 store(i - 1, 0, H)
             deviation(i)
             if i == 0:
-                regroup(2, 0, nc.scalar.copy, 0, SCALAR_STEPS)
+                regroup(2, 0, nc.scalar.copy, 0, THIRD_SCALAR_STEPS)
             centre_and_gain(i)
         add_squares(UNITS - 1)
         inverse_deviation(UNITS - 1)

@@ -32,9 +32,9 @@ HEAD_COLS = COLS // H
 LAST_PIECES = 4
 
 FIRST_SCALAR_STEPS = 48
-SCALAR_STEPS = 80
+SCALAR_STEPS = 96
 THIRD_SCALAR_STEPS = 48
-VECTOR_BINS = 2
+VECTOR_BINS = 3
 RUN = 4
 
 FLOPS = 2 * OUT_CH * CIN * B * FREQ * T
@@ -313,32 +313,35 @@ def tile_unified2dattentiononframe_pa_t_kernel(
                 scale=rest_t[:, 0:1],
             )
 
-        def turn(i, a):
-            pieces = []
-            for f in range(FREQ):
-                terms = [p_tiles[i][:, a, f, :]]
-                if f >= vector_bins(a):
-                    terms.append(slopes[i][:, a, f * P : (f + 1) * P])
-                pieces.append(terms)
-            flat = [term for terms in pieces for term in terms]
-            for k, term in enumerate(flat):
+        def terms(i, a, f):
+            if f < vector_bins(a):
+                return [p_tiles[i][:, a, f, :]]
+            return [p_tiles[i][:, a, f, :], slopes[i][:, a, f * P : (f + 1) * P]]
+
+        def add_up(i, a):
+            pieces = [term for f in range(FREQ) for term in terms(i, a, f)]
+            for k, term in enumerate(pieces):
                 nc.tensor.matmul(
                     out=total,
                     lhsT=term,
                     rhs=ident[:],
                     is_transpose=True,
                     start=(a == 0 and k == 0),
-                    stop=(a == O_STRIPES - 1 and k == len(flat) - 1),
+                    stop=(a == O_STRIPES - 1 and k == len(pieces) - 1),
                 )
-            for f, terms in enumerate(pieces):
-                for k, term in enumerate(terms):
+
+        def turn(i, a):
+            pt = pt_pool.tile([P, FREQ, P], F32, tag="pt")
+            pt_banks[(i, a)] = pt
+            for f in range(FREQ):
+                for k, term in enumerate(terms(i, a, f)):
                     nc.tensor.matmul(
-                        out=pt_banks[(i, a)][:, f, :],
+                        out=pt[:, f, :],
                         lhsT=term,
                         rhs=ident[:],
                         is_transpose=True,
                         start=(k == 0),
-                        stop=(k == len(terms) - 1),
+                        stop=(k == len(terms(i, a, f)) - 1),
                     )
 
         def mean(i):
@@ -387,8 +390,7 @@ def tile_unified2dattentiononframe_pa_t_kernel(
                     op0=ALU.add,
                     op1=ALU.mult,
                 )
-                if a != 1:
-                    keep_warm(unread, n[:, a * BANK : a * BANK + P])
+                keep_warm(unread, n[:, a * BANK : a * BANK + P])
 
         def scale_and_shift(i, first_head, end_head):
             n = n_tiles[i]
@@ -433,13 +435,16 @@ def tile_unified2dattentiononframe_pa_t_kernel(
             if i > 0:
                 inverse_deviation(i - 1)
             slope_branch(i, 2)
-            for a in range(O_STRIPES):
-                pt = pt_pool.tile([P, FREQ, P], F32, tag="pt")
-                pt_banks[(i, a)] = pt
             rest_branch(i, O_STRIPES - 1)
-            for a in range(O_STRIPES):
-                prelu(i, a)
-                turn(i, a)
+            prelu(i, 0)
+            add_up(i, 0)
+            turn(i, 0)
+            prelu(i, 1)
+            add_up(i, 1)
+            prelu(i, 2)
+            add_up(i, 2)
+            turn(i, 1)
+            turn(i, 2)
             if i + 2 < UNITS:
                 b_next, tt_next = divmod(i + 2, T_STRIPES)
                 if tt_next == 0 and b_next + 1 < B:

from contextlib import ExitStack

import concourse.mybir as mybir
from concourse.masks import make_identity

F32 = mybir.dt.float32
BF16 = mybir.dt.bfloat16
U32 = mybir.dt.uint32
U8 = mybir.dt.uint8
FP8X4 = mybir.dt.float8_e4m3fn_x4
ALU = mybir.AluOpType
ACT = mybir.ActivationFunctionType

B, CIN, HID, FREQ, T, H = 4, 1024, 128, 4, 512, 8
OUT_CH = 3 * HID
HD = HID * FREQ // H
EPS = 1e-5

P = 128
PACK = 4
K_PASS = P * PACK
PASSES = CIN // K_PASS
PAIRS = PACK // 2
O_STRIPES = OUT_CH // P
T_STRIPES = T // P
UNITS = B * T_STRIPES
COLS = OUT_CH * FREQ
BANK = 512
BANKS = COLS // BANK
HEAD_COLS = COLS // H

LAST_PIECES = 4

FIRST_SCALAR_STEPS = 48
SCALAR_STEPS = 96
THIRD_SCALAR_STEPS = 48
VECTOR_BINS = 3
RUN = 4

FLOPS = 2 * OUT_CH * CIN * B * FREQ * T

ROW_BIAS = 0
ROW_ALPHA = OUT_CH

HEAD_WARM = 4


def tile_unified2dattentiononframe_pa_t_kernel(
    tc, x, qkv_w, qkv_b, qkv_alpha, qkv_gamma, qkv_beta, out_0, out_1, out_2
):
    nc = tc.nc
    outs = (out_0, out_1, out_2)
    with ExitStack() as ctx:
        const = ctx.enter_context(tc.tile_pool(name="const", bufs=1))
        raw_pool = ctx.enter_context(tc.tile_pool(name="raw", bufs=2 * PASSES))
        grouped_pool = ctx.enter_context(tc.tile_pool(name="grouped", bufs=2))
        grouped_late_pool = ctx.enter_context(tc.tile_pool(name="grouped_late", bufs=1))
        code_pool = ctx.enter_context(tc.tile_pool(name="codes", bufs=3))
        slope_pool = ctx.enter_context(tc.tile_pool(name="slope", bufs=2))
        p_pool = ctx.enter_context(tc.tile_pool(name="p", bufs=2))
        n_pool = ctx.enter_context(tc.tile_pool(name="n", bufs=8))
        small = ctx.enter_context(tc.tile_pool(name="small", bufs=4))
        square_pool = ctx.enter_context(tc.tile_pool(name="square", bufs=2))
        z_pool = ctx.enter_context(tc.psum_pool(name="z", bufs=BANKS))
        pt_pool = ctx.enter_context(tc.psum_pool(name="pt", bufs=BANKS))
        keep_pool = ctx.enter_context(tc.psum_pool(name="keep", bufs=1))
        ctx.enter_context(tc.manual_schedule())

        raw = {}

        def new_x_tiles(b):
            for g in range(PASSES):
                chunk = raw_pool.tile([P, PACK, FREQ, T], BF16, tag="raw", name="chunk")
                raw[(b, g)] = chunk

        def load_x(b, t_range):
            for g in range(PASSES):
                nc.sync.dma_start(
                    out=raw[(b, g)][:, :, :, t_range],
                    in_=x[b, g * K_PASS : (g + 1) * K_PASS, :, t_range].rearrange("(p j) f t -> p j f t", j=PACK),
                )

        rows = const.tile([P, BANK], BF16)
        nc.gpsimd.memset(rows[:].bitcast(U32), 0)
        beta_row = const.tile([P, COLS], BF16)
        nc.gpsimd.memset(beta_row[:].bitcast(U32), 0)
        ones = const.tile([P, P], BF16)
        nc.vector.memset(ones[:], 1.0)
        eps_t = const.tile([P, 1], F32)
        nc.vector.memset(eps_t[:], EPS)
        gamma_row = const.tile([P, COLS], BF16)
        nc.vector.memset(gamma_row[:], 0.0)
        w_sb = const.tile([P, O_STRIPES * CIN], BF16)
        nc.sync.dma_start(out=rows[0:1, ROW_ALPHA : ROW_ALPHA + 1], in_=qkv_alpha.rearrange("(r o) -> r o", r=1))
        nc.sync.dma_start(out=rows[0:1, ROW_BIAS : ROW_BIAS + OUT_CH], in_=qkv_b.rearrange("(r o) -> r o", r=1))
        for a in range(O_STRIPES):
            nc.sync.dma_start(out=w_sb[:, a * CIN : (a + 1) * CIN], in_=qkv_w[a * P : (a + 1) * P, :])
        nc.sync.dma_start(out=beta_row[0:1, :], in_=qkv_beta.rearrange("r o c f -> r (o c f)"))
        nc.sync.dma_start(out=gamma_row[0:1, :], in_=qkv_gamma.rearrange("r o c f -> r (o c f)"))
        new_x_tiles(0)
        for tt in range(T_STRIPES):
            load_x(0, slice(tt * P, (tt + 1) * P))
        new_x_tiles(1)
        for half in range(2):
            load_x(1, slice(half * T // 2, (half + 1) * T // 2))

        warm = const.tile([P, 1], F32)
        nc.scalar.activation(out=warm[:], in_=eps_t[:], func=ACT.Abs_reciprocal_sqrt)

        ident = const.tile([P, P], F32)
        make_identity(nc, ident[:])
        warm_copy = const.tile([P, 1], F32)
        nc.gpsimd.tensor_scalar(out=warm_copy[:], in0=ident[:, 0:1], scalar1=1.0, scalar2=0.0, op0=ALU.mult, op1=ALU.add)

        beta_bank = keep_pool.tile([P, 2, BANK], BF16, tag="beta_bank")
        sums_bank = keep_pool.tile([P, FREQ, P], F32, tag="sums_bank")
        total = sums_bank[:, 0, :]
        unread = sums_bank[:, 1, :]

        def keep_warm(out, tile_ap):
            nc.tensor.matmul(out=out, lhsT=ident[:], rhs=tile_ap, start=True, stop=True)

        for k in range(HEAD_WARM):
            keep_warm(unread, ident[:])

        w_pairs = w_sb[:].bitcast(F32).rearrange("p (a g q u) -> p a g q u", a=O_STRIPES, g=PASSES, q=P, u=PAIRS)
        w_grouped = const.tile([P, PASSES * OUT_CH * PACK], BF16, align_bytes=64)
        w_grouped_pairs = w_grouped[:].bitcast(F32).rearrange("p (g o u) -> p g o u", g=PASSES, o=OUT_CH, u=PAIRS)
        w_signed = const.tile([P, PASSES * OUT_CH * PACK], BF16, align_bytes=64)
        w_codes = const.tile([P, PASSES, OUT_CH], U32, align_bytes=64)
        w_scales = const.tile([P, PASSES, OUT_CH], U8, align_bytes=64)
        alpha_t = const.tile([P, 1], F32)
        sign = const.tile([P, 1], F32)
        signed_ones = const.tile([P, P], BF16)
        bias_col = const.tile([P, O_STRIPES], F32)
        slope_bias_col = const.tile([P, O_STRIPES], F32)
        rest_t = const.tile([P, 1], F32)
        rest_bias_col = const.tile([P, O_STRIPES], F32)

        def turn_weights(k):
            a, g = divmod(k, PASSES)
            wt = z_pool.tile([P, PAIRS, P], F32, tag="z", name="wt")
            for u in range(PAIRS):
                nc.tensor.transpose(wt[:, u, :], w_pairs[:, a, g, :, u], ident[:])
            nc.vector.tensor_copy(
                out=w_grouped_pairs[:, g, a * P : (a + 1) * P, :], in_=wt[:].rearrange("p u o -> p o u")
            )

        def sign_weights(k):
            a, g = divmod(k, PASSES)
            first = (g * OUT_CH + a * P) * PACK
            block = slice(first, first + P * PACK)
            nc.vector.tensor_scalar(
                out=w_signed[:, block], in0=w_grouped[:, block], scalar1=sign[:, 0:1], scalar2=None, op0=ALU.mult
            )

        def quantise_weights(k):
            a, g = divmod(k, PASSES)
            first = (g * OUT_CH + a * P) * PACK
            nc.vector.quantize_mx(
                out=w_codes[:, g, a * P : (a + 1) * P].bitcast(FP8X4),
                scales=w_scales[:, g, a * P : (a + 1) * P],
                in_=w_signed[:, first : first + P * PACK],
            )

        def spread(out, factor, row):
            nc.tensor.matmul(out=out, lhsT=factor[:], rhs=row, start=True, stop=True)

        def find_sign():
            bias_bank = pt_pool.tile([P, BANK], F32, tag="pt")
            spread(bias_bank[:], ones, rows[:])
            nc.vector.tensor_copy(out=alpha_t[:], in_=bias_bank[:, ROW_ALPHA : ROW_ALPHA + 1])
            nc.vector.tensor_scalar(out=sign[:], in0=alpha_t[:], scalar1=1.0, scalar2=2.0, op0=ALU.is_le, op1=ALU.mult)
            nc.vector.tensor_scalar(out=sign[:], in0=sign[:], scalar1=-1.0, scalar2=None, op0=ALU.add)
            nc.vector.tensor_scalar(out=signed_ones[:], in0=ones[:], scalar1=sign[:, 0:1], scalar2=None, op0=ALU.mult)

        turn_weights(0)
        turn_weights(1)
        find_sign()
        blocks = O_STRIPES * PASSES
        for k in range(2, blocks + 2):
            if k < blocks:
                turn_weights(k)
            sign_weights(k - 2)
            if k > 2:
                quantise_weights(k - 3)
        bias_cols_bank = pt_pool.tile([P, BANK], F32, tag="pt")
        for a in range(O_STRIPES):
            nc.tensor.matmul(
                out=bias_cols_bank[:, a : a + 1],
                lhsT=rows[:, ROW_BIAS + a * P : ROW_BIAS + (a + 1) * P],
                rhs=signed_ones[:, 0:1],
                start=True,
                stop=True,
            )
        nc.vector.tensor_copy(out=bias_col[:], in_=bias_cols_bank[:, 0:O_STRIPES])
        quantise_weights(blocks - 1)
        nc.vector.tensor_scalar(out=rest_t[:], in0=alpha_t[:], scalar1=-1.0, scalar2=1.0, op0=ALU.mult, op1=ALU.add)
        for out, factor in ((slope_bias_col, alpha_t), (rest_bias_col, rest_t)):
            nc.vector.tensor_scalar(out=out[:], in0=bias_col[:], scalar1=factor[:, 0:1], scalar2=None, op0=ALU.mult)

        for k in range(2):
            spread(beta_bank[:, k, :], ones, beta_row[:, k * BANK : (k + 1) * BANK])
        table = const.tile([P, 4, BANK], BF16)
        gamma_t = table[:, 0:BANKS, :].rearrange("p k c -> p (k c)")
        beta_end = table[:, BANKS, :]
        table_banks = []
        for first in range(0, 4, 2):
            bank = pt_pool.tile([P, 2, BANK], BF16, tag="pt", name="bank")
            for k in range(first, first + 2):
                if k < BANKS:
                    spread(bank[:, k - first, :], signed_ones, gamma_row[:, k * BANK : (k + 1) * BANK])
                else:
                    spread(bank[:, k - first, :], ones, beta_row[:, 2 * BANK : 3 * BANK])
            table_banks.append(bank)

        def copy_table(copy):
            for k, bank in enumerate(table_banks):
                copy(out=table[:, 2 * k : 2 * k + 2, :], in_=bank[:])

        grouped = {}
        x_codes = {}
        x_scales = {}
        z_banks = {}
        slopes = {}
        p_tiles = {}
        pt_banks = {}
        n_tiles = {}
        neg_means = {}
        squares = {}
        totals_sq = {}
        rstds = {}

        def copy_on_gpsimd(out, in_):
            nc.gpsimd.tensor_scalar(out=out, in0=in_, scalar1=1.0, scalar2=0.0, op0=ALU.mult, op1=ALU.add)

        def regroup(i, g, copy, first_step=0, end_step=P):
            b, tt = divmod(i, T_STRIPES)
            if (i, g) not in grouped:
                pool = grouped_pool if g == 0 else grouped_late_pool
                side = pool.tile([P, FREQ, P, PACK], BF16, tag="grouped", name="side", align_bytes=64)
                grouped[(i, g)] = side
            run = 1 if copy == copy_on_gpsimd else RUN
            copy(
                out=grouped[(i, g)][:, :, first_step:end_step, :].rearrange("p f (c i) j -> p f c j i", i=run),
                in_=raw[(b, g)][:, :, :, tt * P + first_step : tt * P + end_step].rearrange(
                    "p j f (c i) -> p f c j i", i=run
                ),
            )

        def quantise(i, g):
            if g == 0:
                codes = code_pool.tile([P, PASSES, FREQ * P], U32, tag="codes", align_bytes=64)
                scales = code_pool.tile([P, PASSES, FREQ * P], U8, tag="scales", align_bytes=64)
                x_codes[i] = codes
                x_scales[i] = scales
            nc.vector.quantize_mx(
                out=x_codes[i][:, g, :].bitcast(FP8X4),
                scales=x_scales[i][:, g, :],
                in_=grouped[(i, g)][:].rearrange("p f t j -> p (f t j)"),
            )

        def multiply(i, g):
            for a in range(O_STRIPES):
                if g == 0:
                    z = z_pool.tile([P, BANK], F32, tag="z")
                    z_banks[(i, a)] = z
                nc.tensor.matmul_mx(
                    out=z_banks[(i, a)][:],
                    lhsT=w_codes[:, g, a * P : (a + 1) * P].bitcast(FP8X4),
                    lhsT_scale=w_scales[:, g, a * P : (a + 1) * P],
                    rhs=x_codes[i][:, g, :].bitcast(FP8X4),
                    rhs_scale=x_scales[i][:, g, :],
                    start=(g == 0),
                    stop=(g == PASSES - 1),
                )

        def slope_branch(i, a):
            if a == 0:
                slope = slope_pool.tile([P, O_STRIPES, BANK], F32, tag="slope")
                slopes[i] = slope
                p_tile = p_pool.tile([P, O_STRIPES, FREQ, P], F32, tag="p")
                p_tiles[i] = p_tile
            nc.scalar.activation(
                out=slopes[i][:, a, :],
                in_=z_banks[(i, a)][:],
                func=ACT.Identity,
                bias=slope_bias_col[:, a : a + 1],
                scale=alpha_t[:, 0:1],
            )

        def vector_bins(a):
            return VECTOR_BINS if a == O_STRIPES - 1 else FREQ

        def prelu(i, a):
            bins = vector_bins(a)
            nc.vector.scalar_tensor_tensor(
                out=p_tiles[i][:, a, 0:bins, :].rearrange("p f t -> p (f t)"),
                in0=z_banks[(i, a)][:, 0 : bins * P],
                scalar=bias_col[:, a : a + 1],
                in1=slopes[i][:, a, 0 : bins * P],
                op0=ALU.add,
                op1=ALU.max,
            )

        def rest_branch(i, a):
            bins = vector_bins(a)
            nc.scalar.activation(
                out=p_tiles[i][:, a, bins:FREQ, :].rearrange("p f t -> p (f t)"),
                in_=z_banks[(i, a)][:, bins * P : FREQ * P],
                func=ACT.Relu,
                bias=rest_bias_col[:, a : a + 1],
                scale=rest_t[:, 0:1],
            )

        def terms(i, a, f):
            if f < vector_bins(a):
                return [p_tiles[i][:, a, f, :]]
            return [p_tiles[i][:, a, f, :], slopes[i][:, a, f * P : (f + 1) * P]]

        def add_up(i, a):
            pieces = [term for f in range(FREQ) for term in terms(i, a, f)]
            for k, term in enumerate(pieces):
                nc.tensor.matmul(
                    out=total,
                    lhsT=term,
                    rhs=ident[:],
                    is_transpose=True,
                    start=(a == 0 and k == 0),
                    stop=(a == O_STRIPES - 1 and k == len(pieces) - 1),
                )

        def turn(i, a):
            pt = pt_pool.tile([P, FREQ, P], F32, tag="pt")
            pt_banks[(i, a)] = pt
            for f in range(FREQ):
                for k, term in enumerate(terms(i, a, f)):
                    nc.tensor.matmul(
                        out=pt[:, f, :],
                        lhsT=term,
                        rhs=ident[:],
                        is_transpose=True,
                        start=(k == 0),
                        stop=(k == len(terms(i, a, f)) - 1),
                    )

        def mean(i):
            neg_mean = small.tile([P, 1], F32, tag="neg_mean")
            folded = square_pool.tile([P, P], F32, tag="folded")
            nc.scalar.activation(out=folded[:], in_=total, func=ACT.Copy, scale=-1.0 / COLS, accum_out=neg_mean[:])
            neg_means[i] = neg_mean

        def deviation(i):
            parts = small.tile([P, O_STRIPES], F32, tag="parts")
            squares[i] = parts
            for a in range(O_STRIPES):
                square = square_pool.tile([P, BANK], BF16, tag="square")
                nc.scalar.activation(
                    out=square[:],
                    in_=pt_banks[(i, a)][:].rearrange("p f o -> p (f o)"),
                    func=ACT.Square,
                    bias=neg_means[i][:, 0:1],
                    scale=1.0,
                    accum_out=parts[:, a : a + 1],
                )

        def add_squares(i):
            total_sq = small.tile([P, 1], F32, tag="total_sq")
            parts_copy = small.tile([P, O_STRIPES], F32, tag="parts_copy")
            nc.scalar.activation(out=parts_copy[:], in_=squares[i][:], func=ACT.Copy, accum_out=total_sq[:])
            totals_sq[i] = total_sq

        def inverse_deviation(i):
            rstd = small.tile([P, 1], F32, tag="rstd")
            nc.scalar.activation(
                out=rstd[:], in_=totals_sq[i][:], func=ACT.Abs_reciprocal_sqrt, bias=eps_t[:, 0:1], scale=1.0 / COLS
            )
            rstds[i] = rstd

        def centre_and_gain(i):
            n = n_pool.tile([P, COLS], F32, tag="n")
            n_tiles[i] = n
            for a in range(O_STRIPES):
                cols = slice(a * BANK, (a + 1) * BANK)
                nc.vector.scalar_tensor_tensor(
                    out=n[:, cols].rearrange("p (o f) -> p o f", f=FREQ),
                    in0=pt_banks[(i, a)][:].rearrange("p f o -> p o f"),
                    scalar=neg_means[i][:, 0:1],
                    in1=gamma_t[:, cols].rearrange("p (o f) -> p o f", f=FREQ),
                    op0=ALU.add,
                    op1=ALU.mult,
                )
                keep_warm(unread, n[:, a * BANK : a * BANK + P])

        def scale_and_shift(i, first_head, end_head):
            n = n_tiles[i]
            for bank, first_col in ((beta_end, 2 * BANK), (beta_bank[:].rearrange("p s c -> p (s c)"), 0)):
                first = max(first_head * HEAD_COLS, first_col)
                end = min(end_head * HEAD_COLS, min(first_col + 2 * BANK, COLS))
                if first < end:
                    nc.vector.scalar_tensor_tensor(
                        out=n[:, first:end],
                        in0=n[:, first:end],
                        scalar=rstds[i][:, 0:1],
                        in1=bank[:, first - first_col : end - first_col],
                        op0=ALU.mult,
                        op1=ALU.add,
                    )

        def store(i, first_head, end_head):
            b, tt = divmod(i, T_STRIPES)
            heads = n_tiles[i][:].rearrange("p (h s d) -> p h s d", h=H, s=len(outs), d=HD)
            for s, out in enumerate(outs):
                nc.sync.dma_start(
                    out=out[b, first_head:end_head, tt * P : (tt + 1) * P, :].rearrange("h t d -> t h d"),
                    in_=heads[:, first_head:end_head, s, :],
                )

        regroup(0, 0, nc.scalar.copy)
        quantise(0, 0)
        multiply(0, 0)
        regroup(0, 1, nc.scalar.copy, 0, FIRST_SCALAR_STEPS)
        regroup(0, 1, nc.vector.tensor_copy, FIRST_SCALAR_STEPS, P)
        copy_table(nc.scalar.copy)
        quantise(0, 1)
        multiply(0, 1)
        regroup(1, 0, nc.vector.tensor_copy)

        for i in range(UNITS):
            slope_branch(i, 0)
            keep_warm(unread, slopes[i][:, 0, 0:P])
            if i > 0:
                add_squares(i - 1)
            slope_branch(i, 1)
            if i > 0:
                inverse_deviation(i - 1)
            slope_branch(i, 2)
            rest_branch(i, O_STRIPES - 1)
            prelu(i, 0)
            add_up(i, 0)
            turn(i, 0)
            prelu(i, 1)
            add_up(i, 1)
            prelu(i, 2)
            add_up(i, 2)
            turn(i, 1)
            turn(i, 2)
            if i + 2 < UNITS:
                b_next, tt_next = divmod(i + 2, T_STRIPES)
                if tt_next == 0 and b_next + 1 < B:
                    new_x_tiles(b_next + 1)
                    load_x(b_next + 1, slice(0, T))
                if i > 0:
                    regroup(i + 2, 0, nc.scalar.copy, 0, SCALAR_STEPS)
            if i == 0:
                regroup(1, 1, nc.scalar.copy, 0, P // 2)
                regroup(1, 1, nc.vector.tensor_copy, P // 2, P)
            if i + 1 < UNITS:
                quantise(i + 1, 0)
                multiply(i + 1, 0)
                quantise(i + 1, 1)
                multiply(i + 1, 1)
            if i + 2 < UNITS:
                if i == 0:
                    regroup(2, 0, copy_on_gpsimd, THIRD_SCALAR_STEPS, P)
                regroup(i + 2, 1, copy_on_gpsimd)
                if i > 0:
                    regroup(i + 2, 0, copy_on_gpsimd, SCALAR_STEPS, P)
            mean(i)
            if i > 0:
                scale_and_shift(i - 1, 0, H)
                keep_warm(unread, n_tiles[i - 1][:, 0:P])
                store(i - 1, 0, H)
            deviation(i)
            if i == 0:
                regroup(2, 0, nc.scalar.copy, 0, THIRD_SCALAR_STEPS)
            centre_and_gain(i)
        add_squares(UNITS - 1)
        inverse_deviation(UNITS - 1)
        for piece in range(LAST_PIECES):
            first_head = piece * H // LAST_PIECES
            end_head = (piece + 1) * H // LAST_PIECES
            scale_and_shift(UNITS - 1, first_head, end_head)
            store(UNITS - 1, first_head, end_head)
